import numpy as np
import ml_dtypes


def mxq(x, axis, fmt="e4m3"):
    dtype, down = {"e4m3": (ml_dtypes.float8_e4m3fn, 7), "e5m2": (ml_dtypes.float8_e5m2, 14)}[fmt]
    v = np.moveaxis(np.asarray(x, np.float32).astype(ml_dtypes.bfloat16).astype(np.float64), axis, -1)
    blocks = v.reshape(v.shape[:-1] + (-1, 32))
    amax = np.abs(blocks).max(-1, keepdims=True)
    byte = np.maximum(np.where(amax > 0, np.frexp(amax)[1] - 1 + 127, 0) - down, 1)
    scale = np.exp2(byte - 127.0)
    codes = (blocks / scale).astype(np.float32).astype(dtype).astype(np.float64)
    return np.moveaxis((codes * scale).reshape(v.shape), -1, axis)


WIDE = False


def mx_kscale(k):
    if not WIDE:
        return np.ones(k)
    levels = np.array([10, -10, 5, -5, 0])
    if k % 512:
        return np.exp2(np.random.permutation(np.resize(levels, k // 32))).repeat(32)
    a = np.empty((k // 512, 16))
    for p in range(k // 512):
        a[p, :8] = np.random.permutation(np.resize(levels, 8))
        for g in range(8):
            far = levels[np.abs(levels - a[p, g]) >= 10]
            a[p, g + 8] = far[np.random.randint(len(far))]
    return np.exp2(a.ravel()).repeat(32)


BF16 = ml_dtypes.bfloat16


def bf(x):
    return np.asarray(x, np.float32).astype(BF16)


def f64(x):
    return np.asarray(x).astype(np.float64)


B, S, D, W = 1, 4096, 128, 512
NB = S // W
MASK_VALUE = -3.4028234663852886e38


def with_prev(cur, prev, op):
    return np.concatenate([cur[:, :1], op(cur[:, 1:], prev)], axis=1)


def setup_inputs():
    t = mx_kscale(W)
    top = t.max()
    f = np.concatenate([np.full(W, top), np.tile(t, NB - 1)])
    q = np.random.standard_normal((B, S, D)) * 2.0
    k = np.random.standard_normal((B, S, D))
    v = np.random.standard_normal((B, S, D)) * (top / f)[:, None]
    q[..., 0] = 8.0
    k[..., 0] += np.log(f) / (8.0 * D ** -0.5)
    return {"q": bf(q), "k": bf(k), "v": bf(v)}


def reference(q, k, v):
    scale = D ** -0.5
    qb = f64(q).reshape(B, NB, W, D)
    kt = f64(k).reshape(B, NB, W, D).transpose(0, 1, 3, 2)
    vq = mxq(f64(v).reshape(B, NB, W, D), 2, "e4m3")
    a = np.arange(W)[:, None]
    c = np.arange(W)[None, :]
    sc = np.where(c <= a, qb @ kt * scale, MASK_VALUE)
    sp = np.where(c > a, qb[:, 1:] @ kt[:, :-1] * scale, MASK_VALUE)
    m = with_prev(sc.max(-1, keepdims=True), sp.max(-1, keepdims=True), np.maximum)
    ec = np.exp(sc - m)
    ep = np.exp(sp - m[:, 1:])
    num = with_prev(mxq(ec, 3, "e4m3") @ vq, mxq(ep, 3, "e4m3") @ vq[:, :-1], np.add)
    den = with_prev(ec.sum(-1, keepdims=True), ep.sum(-1, keepdims=True), np.add)
    return (num / den).reshape(B, S, D)

@@ -1,0 +1,285 @@
+from contextlib import ExitStack
+
+import concourse.mybir as mybir
+from concourse.masks import make_identity
+
+F32 = mybir.dt.float32
+BF16 = mybir.dt.bfloat16
+U32 = mybir.dt.uint32
+U8 = mybir.dt.uint8
+FP8X4 = mybir.dt.float8_e4m3fn_x4
+ALU = mybir.AluOpType
+ACT = mybir.ActivationFunctionType
+AXIS = mybir.AxisListType
+
+P = 128
+S = 4096
+D = 128
+PACK = 4
+BLOCK = PACK * P
+TILES = S // P
+BLOCKS = S // BLOCK
+SCALE = D ** -0.5
+MASKED = -3.0e38
+
+FLOPS = 2 * (2 * BLOCKS - 1) * 2 * BLOCK * BLOCK * D
+
+
+def tile_exactslidingwindowattention_kernel(tc, q, k, v, out):
+    nc = tc.nc
+    q_blocks = q.flatten_outer_dims().rearrange("(n t p) d -> n p t d", t=PACK, p=P)
+    k_blocks = k.flatten_outer_dims().rearrange("(n t p) d -> n p t d", t=PACK, p=P)
+    v_blocks = v.flatten_outer_dims().rearrange("(n p t) d -> n p t d", t=PACK, p=P)
+    out_blocks = out.flatten_outer_dims().rearrange("(n t p) d -> n p t d", t=PACK, p=P)
+
+    with ExitStack() as ctx:
+        ctx.enter_context(tc.manual_schedule())
+        keep = ctx.enter_context(tc.tile_pool(name="keep", bufs=1))
+        work = ctx.enter_context(tc.tile_pool(name="work", bufs=4))
+        per_block = ctx.enter_context(tc.tile_pool(name="per_block", bufs=2))
+        small = ctx.enter_context(tc.tile_pool(name="small", bufs=4))
+        psum_window = ctx.enter_context(tc.psum_pool(name="psum_window", bufs=2))
+        psum_diag = ctx.enter_context(tc.psum_pool(name="psum_diag", bufs=2))
+        psum_eT = ctx.enter_context(tc.psum_pool(name="psum_eT", bufs=2))
+        psum_num = ctx.enter_context(tc.psum_pool(name="psum_num", bufs=1))
+        psum_qkT = ctx.enter_context(tc.psum_pool(name="psum_qkT", bufs=1))
+
+        q_sb = keep.tile([P, BLOCKS, PACK, D], BF16)
+        k_sb = keep.tile([P, BLOCKS, PACK, D], BF16)
+        v_sb = keep.tile([P, BLOCKS, PACK, D], BF16)
+
+        def load_v(n):
+            nc.sync.dma_start(out=v_sb[:, n], in_=v_blocks[n])
+
+        for n in range(BLOCKS):
+            nc.sync.dma_start(out=k_sb[:, n], in_=k_blocks[n])
+            nc.sync.dma_start(out=q_sb[:, n], in_=q_blocks[n])
+            if n > 0:
+                load_v(n - 1)
+        load_v(BLOCKS - 1)
+
+        e_win = []
+        for r in range(PACK):
+            e_win_r = keep.tile([P, 2 * BLOCK], BF16, name="e_win%d" % r)
+            nc.vector.memset(e_win_r[:], 0.0)
+            e_win.append(e_win_r)
+        den_parts = keep.tile([P, BLOCKS, PACK, 2], F32)
+        nc.vector.memset(den_parts[:], 0.0)
+
+        ident = keep.tile([P, P], BF16)
+        make_identity(nc, ident[:])
+        ident_f32 = keep.tile([P, P], F32)
+        make_identity(nc, ident_f32[:])
+        mask_own_f32 = keep.tile([P, P], F32)
+        nc.gpsimd.memset(mask_own_f32[:], 0.0)
+        nc.gpsimd.affine_select(
+            out=mask_own_f32[:], in_=mask_own_f32[:], compare_op=ALU.is_ge, fill=MASKED,
+            base=0, pattern=[[-1, P]], channel_multiplier=1,
+        )
+        mask_prev_f32 = keep.tile([P, P], F32)
+        nc.gpsimd.memset(mask_prev_f32[:], 0.0)
+        nc.gpsimd.affine_select(
+            out=mask_prev_f32[:], in_=mask_prev_f32[:], compare_op=ALU.is_ge, fill=MASKED,
+            base=-1, pattern=[[1, P]], channel_multiplier=-1,
+        )
+        mask_own = keep.tile([P, P], BF16)
+        nc.vector.tensor_copy(out=mask_own[:], in_=mask_own_f32[:])
+        mask_prev = keep.tile([P, P], BF16)
+        nc.vector.tensor_copy(out=mask_prev[:], in_=mask_prev_f32[:])
+
+        kqT = keep.tile([D, 2, S], BF16)
+        kT = kqT[:, 0, :]
+        qT = kqT[:, 1, :]
+        v_codes = keep.tile([P, BLOCKS, D], U32, align_bytes=64)
+        v_scales = keep.tile([P, BLOCKS, D], U8, align_bytes=64)
+
+        diag_ps = {}
+        diag_max = {}
+        window_ps = {}
+        window_max = {}
+        neg_max = {}
+        v_grouped = {}
+        den = {}
+        inv_den = {}
+        num_ps = {}
+        grouped = {}
+        e_codes = {}
+        e_scales = {}
+
+        def first_key_tile(T):
+            return max(T - PACK, 0)
+
+        def first_side(n):
+            return 0 if n > 0 else 1
+
+        def prepare_qk(n):
+            kqT_ps = psum_qkT.tile([D, 2, PACK, P], BF16)
+            for t in range(PACK):
+                nc.tensor.transpose(kqT_ps[:, 0, t, :], k_sb[:, n, t, :], ident[:])
+            for t in range(PACK):
+                nc.tensor.transpose(kqT_ps[:, 1, t, :], q_sb[:, n, t, :], ident[:])
+            nc.scalar.copy(out=kqT[:, :, n * BLOCK:(n + 1) * BLOCK],
+                           in_=kqT_ps[:].rearrange("d h t p -> d h (t p)"))
+
+        def v_regrouped(n):
+            v_grouped[n] = work.tile([P, D, PACK], BF16, name="v_grouped", align_bytes=64)
+            nc.vector.tensor_copy(out=v_grouped[n][:], in_=v_sb[:, n].rearrange("p t d -> p d t"))
+
+        def v_quantised(n):
+            nc.vector.quantize_mx(
+                out=v_codes[:, n, :].bitcast(FP8X4),
+                scales=v_scales[:, n, :],
+                in_=v_grouped[n][:].rearrange("p d t -> p (d t)"),
+            )
+
+        def diagonal_scores(n):
+            diag_ps[n] = psum_diag.tile([P, PACK, P], F32, name="diag_ps")
+            for r in range(PACK):
+                tile_cols = slice((n * PACK + r) * P, (n * PACK + r + 1) * P)
+                nc.tensor.matmul(out=diag_ps[n][:, r, :], lhsT=qT[:, tile_cols],
+                                 rhs=kT[:, tile_cols], start=True, stop=False)
+                nc.tensor.matmul(out=diag_ps[n][:, r, :], lhsT=ident[:], rhs=mask_own[:],
+                                 start=False, stop=True)
+
+        def diagonal_max(n):
+            diag_max[n] = small.tile([P, PACK], F32, name="diag_max")
+            nc.vector.tensor_reduce(out=diag_max[n][:], in_=diag_ps[n][:], axis=AXIS.X, op=ALU.max)
+
+        def window_scores(T):
+            if T == 0:
+                return
+            window_ps[T] = psum_window.tile([P, BLOCK], F32, name="window_ps")
+            clipped = T >= PACK
+            nc.tensor.matmul(out=window_ps[T][:, 0:(T - first_key_tile(T)) * P],
+                             lhsT=qT[:, T * P:(T + 1) * P],
+                             rhs=kT[:, first_key_tile(T) * P:T * P],
+                             start=True, stop=not clipped)
+            if clipped:
+                nc.tensor.matmul(out=window_ps[T][:, 0:P], lhsT=ident[:], rhs=mask_prev[:],
+                                 start=False, stop=True)
+
+        def window_maximum(T):
+            if T > 0:
+                window_max[T] = small.tile([P, 1], F32, name="window_max")
+                nc.vector.tensor_reduce(out=window_max[T][:],
+                                        in_=window_ps[T][:, 0:(T - first_key_tile(T)) * P],
+                                        axis=AXIS.X, op=ALU.max)
+
+        def row_maximum(T):
+            n, r = divmod(T, PACK)
+            neg_max[T] = small.tile([P, 1], F32, name="neg_max")
+            if T > 0:
+                nc.vector.tensor_scalar(out=neg_max[T][:], in0=window_max[T][:],
+                                        scalar1=diag_max[n][:, r:r + 1], scalar2=-SCALE,
+                                        op0=ALU.max, op1=ALU.mult)
+            else:
+                nc.vector.tensor_scalar(out=neg_max[T][:], in0=diag_max[n][:, r:r + 1],
+                                        scalar1=-SCALE, scalar2=None, op0=ALU.mult)
+
+        def exponentials(T):
+            n, r = divmod(T, PACK)
+            width = (T - first_key_tile(T)) * P
+            base = (first_key_tile(T) - (n - 1) * PACK) * P
+            if T > 0:
+                nc.scalar.activation(out=e_win[r][:, base:base + width],
+                                     in_=window_ps[T][:, 0:width],
+                                     func=ACT.Exp, bias=neg_max[T][:], scale=SCALE,
+                                     accum_out=den_parts[:, n, r, 0:1])
+            nc.scalar.activation(out=e_win[r][:, base + width:base + width + P],
+                                 in_=diag_ps[n][:, r, :],
+                                 func=ACT.Exp, bias=neg_max[T][:], scale=SCALE,
+                                 accum_out=den_parts[:, n, r, 1:2])
+
+        def transposed(T):
+            n, r = divmod(T, PACK)
+            eT_ps = psum_eT.tile([P, 2, 2, P], F32)
+            words = e_win[r][:].bitcast(F32)
+            for side in range(first_side(n), 2):
+                for u in range(2):
+                    nc.tensor.transpose(eT_ps[:, side, u, :],
+                                        words[:, 2 * side * P + u:2 * (side + 1) * P:2],
+                                        ident_f32[:])
+            grouped[T] = work.tile([P, 2, P, PACK], BF16, name="grouped", align_bytes=64)
+            nc.scalar.copy(
+                out=grouped[T][:].rearrange("p s q t -> p (s q t)").bitcast(F32).rearrange(
+                    "p (s q u) -> p s q u", s=2, u=2)[:, first_side(n):],
+                in_=eT_ps[:, first_side(n):].rearrange("p s u q -> p s q u"))
+
+        def quantised(T):
+            n, r = divmod(T, PACK)
+            if r == 0:
+                e_codes[n] = per_block.tile([P, PACK, 2 * P], U32, name="e_codes", align_bytes=64)
+                e_scales[n] = per_block.tile([P, PACK, 2 * P], U8, name="e_scales", align_bytes=64)
+            nc.vector.quantize_mx(
+                out=e_codes[n][:, r, first_side(n) * P:].bitcast(FP8X4),
+                scales=e_scales[n][:, r, first_side(n) * P:],
+                in_=grouped[T][:, first_side(n):, :, :].rearrange("p s q t -> p (s q t)"),
+            )
+
+        def product(n):
+            num_ps[n] = psum_num.tile([P, PACK, D], F32, name="num_ps")
+            for r in range(PACK):
+                for side in range(first_side(n), 2):
+                    cols = slice(side * P, (side + 1) * P)
+                    nc.tensor.matmul_mx(
+                        out=num_ps[n][:, r, :],
+                        lhsT=e_codes[n][:, r, cols].bitcast(FP8X4),
+                        lhsT_scale=e_scales[n][:, r, cols],
+                        rhs=v_codes[:, n - 1 + side, :].bitcast(FP8X4),
+                        rhs_scale=v_scales[:, n - 1 + side, :],
+                        start=(side == first_side(n)),
+                        stop=(side == 1),
+                    )
+
+        def row_sums(n):
+            den[n] = small.tile([P, PACK], F32, name="den")
+            nc.vector.tensor_reduce(out=den[n][:], in_=den_parts[:, n], axis=AXIS.X, op=ALU.add)
+
+        def reciprocals(n):
+            inv_den[n] = small.tile([P, PACK], F32, name="inv_den")
+            nc.vector.reciprocal(out=inv_den[n][:], in_=den[n][:])
+
+        def normalised(n):
+            out_sb = per_block.tile([P, PACK, D], F32)
+            nc.vector.tensor_tensor(out=out_sb[:], in0=num_ps[n][:],
+                                    in1=inv_den[n][:].unsqueeze(2).to_broadcast([P, PACK, D]),
+                                    op=ALU.mult)
+            nc.sync.dma_start(out=out_blocks[n], in_=out_sb[:])
+
+        def in_range(x, count):
+            return 0 <= x < count
+
+        prepare_qk(0)
+        diagonal_scores(0)
+        diagonal_max(0)
+        for step in range(-1, TILES + 2 * PACK + 1):
+            n, r = divmod(step, PACK)
+            if in_range(step + 1, TILES):
+                window_scores(step + 1)
+            if in_range(step, TILES):
+                window_maximum(step)
+            if in_range(step - 3, TILES):
+                quantised(step - 3)
+            if in_range(step, TILES):
+                row_maximum(step)
+                exponentials(step)
+            if in_range(step - 1, TILES):
+                transposed(step - 1)
+            if r == 0 and in_range(n + 1, BLOCKS):
+                prepare_qk(n + 1)
+            if r == 0 and in_range(n - 1, BLOCKS):
+                v_quantised(n - 1)
+            if r == 0 and in_range(n - 2, BLOCKS):
+                normalised(n - 2)
+            if r == 1 and in_range(n + 1, BLOCKS):
+                diagonal_scores(n + 1)
+            if r == 1 and in_range(n - 1, BLOCKS):
+                row_sums(n - 1)
+            if r == 2 and in_range(n + 1, BLOCKS):
+                diagonal_max(n + 1)
+            if r == 2 and in_range(n - 1, BLOCKS):
+                reciprocals(n - 1)
+            if r == 3 and in_range(n, BLOCKS):
+                v_regrouped(n)
+            if r == 3 and in_range(n - 1, BLOCKS):
+                product(n - 1)

@@ -6,6 +6,7 @@ from concourse.masks import make_identity
 F32 = mybir.dt.float32
 BF16 = mybir.dt.bfloat16
 U32 = mybir.dt.uint32
+I32 = mybir.dt.int32
 U8 = mybir.dt.uint8
 FP8X4 = mybir.dt.float8_e4m3fn_x4
 ALU = mybir.AluOpType
@@ -17,8 +18,10 @@ S = 4096
 D = 128
 PACK = 4
 BLOCK = PACK * P
+SLOT = P // PACK
 TILES = S // P
 BLOCKS = S // BLOCK
+SEEN = PACK + 1
 SCALE = D ** -0.5
 MASKED = -3.0e38
 
@@ -38,33 +41,20 @@ def tile_exactslidingwindowattention_kernel(tc, q, k, v, out):
         work = ctx.enter_context(tc.tile_pool(name="work", bufs=4))
         per_block = ctx.enter_context(tc.tile_pool(name="per_block", bufs=2))
         small = ctx.enter_context(tc.tile_pool(name="small", bufs=4))
-        psum_window = ctx.enter_context(tc.psum_pool(name="psum_window", bufs=2))
+        psum_window = ctx.enter_context(tc.psum_pool(name="psum_window", bufs=3))
         psum_diag = ctx.enter_context(tc.psum_pool(name="psum_diag", bufs=2))
         psum_eT = ctx.enter_context(tc.psum_pool(name="psum_eT", bufs=2))
-        psum_num = ctx.enter_context(tc.psum_pool(name="psum_num", bufs=1))
-        psum_qkT = ctx.enter_context(tc.psum_pool(name="psum_qkT", bufs=1))
+        psum_turns = ctx.enter_context(tc.psum_pool(name="psum_turns", bufs=1))
 
         q_sb = keep.tile([P, BLOCKS, PACK, D], BF16)
         k_sb = keep.tile([P, BLOCKS, PACK, D], BF16)
         v_sb = keep.tile([P, BLOCKS, PACK, D], BF16)
-
-        def load_v(n):
-            nc.sync.dma_start(out=v_sb[:, n], in_=v_blocks[n])
-
         for n in range(BLOCKS):
             nc.sync.dma_start(out=k_sb[:, n], in_=k_blocks[n])
             nc.sync.dma_start(out=q_sb[:, n], in_=q_blocks[n])
             if n > 0:
-                load_v(n - 1)
-        load_v(BLOCKS - 1)
-
-        e_win = []
-        for r in range(PACK):
-            e_win_r = keep.tile([P, 2 * BLOCK], BF16, name="e_win%d" % r)
-            nc.vector.memset(e_win_r[:], 0.0)
-            e_win.append(e_win_r)
-        den_parts = keep.tile([P, BLOCKS, PACK, 2], F32)
-        nc.vector.memset(den_parts[:], 0.0)
+                nc.sync.dma_start(out=v_sb[:, n - 1], in_=v_blocks[n - 1])
+        nc.sync.dma_start(out=v_sb[:, BLOCKS - 1], in_=v_blocks[BLOCKS - 1])
 
         ident = keep.tile([P, P], BF16)
         make_identity(nc, ident[:])
@@ -82,16 +72,29 @@ def tile_exactslidingwindowattention_kernel(tc, q, k, v, out):
             out=mask_prev_f32[:], in_=mask_prev_f32[:], compare_op=ALU.is_ge, fill=MASKED,
             base=-1, pattern=[[1, P]], channel_multiplier=-1,
         )
+
         mask_own = keep.tile([P, P], BF16)
         nc.vector.tensor_copy(out=mask_own[:], in_=mask_own_f32[:])
         mask_prev = keep.tile([P, P], BF16)
         nc.vector.tensor_copy(out=mask_prev[:], in_=mask_prev_f32[:])
 
-        kqT = keep.tile([D, 2, S], BF16)
-        kT = kqT[:, 0, :]
-        qT = kqT[:, 1, :]
+        e_row = []
+        for n in range(BLOCKS):
+            e_row_n = keep.tile([P, PACK * SEEN, P], BF16, name="e_row%d" % n)
+            e_row.append(e_row_n)
+        for r in range(1, PACK):
+            nc.vector.memset(e_row[0][:, SEEN * r:SEEN * r + PACK - r, :], 0.0)
+        den_parts = keep.tile([P, BLOCKS, PACK, 2], F32)
+        nc.vector.memset(den_parts[:], 0.0)
+
+        kT = keep.tile([D, S], BF16)
+        qT = keep.tile([D, S], BF16)
         v_codes = keep.tile([P, BLOCKS, D], U32, align_bytes=64)
         v_scales = keep.tile([P, BLOCKS, D], U8, align_bytes=64)
+        variants = 2 * (PACK - 1)
+        v_part = keep.tile([P, BLOCKS, variants, D], U32, align_bytes=64)
+        for n in range(BLOCKS):
+            nc.gpsimd.memset(v_part[:, n], 0)
 
         diag_ps = {}
         diag_max = {}
@@ -106,20 +109,23 @@ def tile_exactslidingwindowattention_kernel(tc, q, k, v, out):
         e_codes = {}
         e_scales = {}
 
-        def first_key_tile(T):
-            return max(T - PACK, 0)
+        def earlier_tiles(T):
+            return min(T, PACK)
 
-        def first_side(n):
-            return 0 if n > 0 else 1
+        def transposed_in(x_sb, n):
+            x_ps = psum_turns.tile([D, PACK, P], BF16, name="x_ps", tag="turns")
+            for t in range(PACK):
+                nc.tensor.transpose(x_ps[:, t, :], x_sb[:, n, t, :], ident[:])
+            return x_ps[:].rearrange("d t p -> d (t p)").bitcast(F32)
 
-        def prepare_qk(n):
-            kqT_ps = psum_qkT.tile([D, 2, PACK, P], BF16)
-            for t in range(PACK):
-                nc.tensor.transpose(kqT_ps[:, 0, t, :], k_sb[:, n, t, :], ident[:])
-            for t in range(PACK):
-                nc.tensor.transpose(kqT_ps[:, 1, t, :], q_sb[:, n, t, :], ident[:])
-            nc.scalar.copy(out=kqT[:, :, n * BLOCK:(n + 1) * BLOCK],
-                           in_=kqT_ps[:].rearrange("d h t p -> d h (t p)"))
+        def prepare_k(n):
+            nc.scalar.copy(out=kT[:].bitcast(F32)[:, n * BLOCK // 2:(n + 1) * BLOCK // 2],
+                           in_=transposed_in(k_sb, n))
+
+        def prepare_q(n):
+            copy = nc.vector.tensor_copy if n == 0 else nc.scalar.copy
+            copy(out=qT[:].bitcast(F32)[:, n * BLOCK // 2:(n + 1) * BLOCK // 2],
+                 in_=transposed_in(q_sb, n))
 
         def v_regrouped(n):
             v_grouped[n] = work.tile([P, D, PACK], BF16, name="v_grouped", align_bytes=64)
@@ -131,28 +137,37 @@ def tile_exactslidingwindowattention_kernel(tc, q, k, v, out):
                 scales=v_scales[:, n, :],
                 in_=v_grouped[n][:].rearrange("p d t -> p (d t)"),
             )
+            for s in range(PACK):
+                rows = slice(s * SLOT, (s + 1) * SLOT)
+                nc.sync.dma_start(
+                    out=v_part[rows, n, s:s + PACK - 1, :].bitcast(I32),
+                    in_=v_codes[rows, n, :].bitcast(I32).unsqueeze(1).to_broadcast(
+                        [SLOT, PACK - 1, D]))
 
-        def diagonal_scores(n):
-            diag_ps[n] = psum_diag.tile([P, PACK, P], F32, name="diag_ps")
-            for r in range(PACK):
-                tile_cols = slice((n * PACK + r) * P, (n * PACK + r + 1) * P)
-                nc.tensor.matmul(out=diag_ps[n][:, r, :], lhsT=qT[:, tile_cols],
-                                 rhs=kT[:, tile_cols], start=True, stop=False)
-                nc.tensor.matmul(out=diag_ps[n][:, r, :], lhsT=ident[:], rhs=mask_own[:],
-                                 start=False, stop=True)
+        def diagonal_scores(n, r):
+            if r == 0:
+                diag_ps[n] = psum_diag.tile([P, PACK, P], F32, name="diag_ps")
+            T = n * PACK + r
+            nc.tensor.matmul(out=diag_ps[n][:, r, :], lhsT=qT[:, T * P:(T + 1) * P],
+                             rhs=kT[:, T * P:(T + 1) * P], start=True, stop=False)
+            nc.tensor.matmul(out=diag_ps[n][:, r, :], lhsT=ident[:], rhs=mask_own[:],
+                             start=False, stop=True)
 
-        def diagonal_max(n):
-            diag_max[n] = small.tile([P, PACK], F32, name="diag_max")
-            nc.vector.tensor_reduce(out=diag_max[n][:], in_=diag_ps[n][:], axis=AXIS.X, op=ALU.max)
+        def diagonal_max(n, r0, r1):
+            if r0 == 0:
+                diag_max[n] = small.tile([P, PACK], F32, name="diag_max")
+            nc.vector.tensor_reduce(out=diag_max[n][:, r0:r1], in_=diag_ps[n][:, r0:r1, :],
+                                    axis=AXIS.X, op=ALU.max)
 
         def window_scores(T):
-            if T == 0:
+            count = earlier_tiles(T)
+            if count == 0:
                 return
             window_ps[T] = psum_window.tile([P, BLOCK], F32, name="window_ps")
-            clipped = T >= PACK
-            nc.tensor.matmul(out=window_ps[T][:, 0:(T - first_key_tile(T)) * P],
+            clipped = count == PACK
+            nc.tensor.matmul(out=window_ps[T][:, 0:count * P],
                              lhsT=qT[:, T * P:(T + 1) * P],
-                             rhs=kT[:, first_key_tile(T) * P:T * P],
+                             rhs=kT[:, (T - count) * P:T * P],
                              start=True, stop=not clipped)
             if clipped:
                 nc.tensor.matmul(out=window_ps[T][:, 0:P], lhsT=ident[:], rhs=mask_prev[:],
@@ -162,7 +177,7 @@ def tile_exactslidingwindowattention_kernel(tc, q, k, v, out):
             if T > 0:
                 window_max[T] = small.tile([P, 1], F32, name="window_max")
                 nc.vector.tensor_reduce(out=window_max[T][:],
-                                        in_=window_ps[T][:, 0:(T - first_key_tile(T)) * P],
+                                        in_=window_ps[T][:, 0:earlier_tiles(T) * P],
                                         axis=AXIS.X, op=ALU.max)
 
         def row_maximum(T):
@@ -178,57 +193,65 @@ def tile_exactslidingwindowattention_kernel(tc, q, k, v, out):
 
         def exponentials(T):
             n, r = divmod(T, PACK)
-            width = (T - first_key_tile(T)) * P
-            base = (first_key_tile(T) - (n - 1) * PACK) * P
+            count = earlier_tiles(T)
+            own = SEEN * r + PACK
             if T > 0:
-                nc.scalar.activation(out=e_win[r][:, base:base + width],
-                                     in_=window_ps[T][:, 0:width],
-                                     func=ACT.Exp, bias=neg_max[T][:], scale=SCALE,
-                                     accum_out=den_parts[:, n, r, 0:1])
-            nc.scalar.activation(out=e_win[r][:, base + width:base + width + P],
-                                 in_=diag_ps[n][:, r, :],
+                nc.scalar.activation(
+                    out=e_row[n][:, own - count:own, :].rearrange("p a c -> p (a c)"),
+                    in_=window_ps[T][:, 0:count * P],
+                    func=ACT.Exp, bias=neg_max[T][:], scale=SCALE,
+                    accum_out=den_parts[:, n, r, 0:1])
+            nc.scalar.activation(out=e_row[n][:, own, :], in_=diag_ps[n][:, r, :],
                                  func=ACT.Exp, bias=neg_max[T][:], scale=SCALE,
                                  accum_out=den_parts[:, n, r, 1:2])
 
-        def transposed(T):
+        def units(T):
             n, r = divmod(T, PACK)
-            eT_ps = psum_eT.tile([P, 2, 2, P], F32)
-            words = e_win[r][:].bitcast(F32)
-            for side in range(first_side(n), 2):
+            done = range((SEEN * r) // PACK, (SEEN * (r + 1)) // PACK)
+            return [(n, w) for w in done if n > 0 or w > 0]
+
+        def transposed(T):
+            for n, w in units(T):
+                eT_ps = psum_eT.tile([P, 2, P], F32, name="eT_ps")
+                words = e_row[n][:].rearrange("p a c -> p (a c)").bitcast(F32)
                 for u in range(2):
-                    nc.tensor.transpose(eT_ps[:, side, u, :],
-                                        words[:, 2 * side * P + u:2 * (side + 1) * P:2],
+                    nc.tensor.transpose(eT_ps[:, u, :], words[:, 2 * w * P + u:2 * (w + 1) * P:2],
                                         ident_f32[:])
-            grouped[T] = work.tile([P, 2, P, PACK], BF16, name="grouped", align_bytes=64)
-            nc.scalar.copy(
-                out=grouped[T][:].rearrange("p s q t -> p (s q t)").bitcast(F32).rearrange(
-                    "p (s q u) -> p s q u", s=2, u=2)[:, first_side(n):],
-                in_=eT_ps[:, first_side(n):].rearrange("p s u q -> p s q u"))
+                grouped[n, w] = work.tile([P, P, PACK], BF16, name="grouped", align_bytes=64)
+                nc.scalar.copy(
+                    out=grouped[n, w][:].rearrange("p q t -> p (q t)").bitcast(F32).rearrange(
+                        "p (q u) -> p q u", u=2),
+                    in_=eT_ps[:].rearrange("p u q -> p q u"))
 
         def quantised(T):
-            n, r = divmod(T, PACK)
-            if r == 0:
-                e_codes[n] = per_block.tile([P, PACK, 2 * P], U32, name="e_codes", align_bytes=64)
-                e_scales[n] = per_block.tile([P, PACK, 2 * P], U8, name="e_scales", align_bytes=64)
-            nc.vector.quantize_mx(
-                out=e_codes[n][:, r, first_side(n) * P:].bitcast(FP8X4),
-                scales=e_scales[n][:, r, first_side(n) * P:],
-                in_=grouped[T][:, first_side(n):, :, :].rearrange("p s q t -> p (s q t)"),
-            )
+            for n, w in units(T):
+                if w == (1 if n == 0 else 0):
+                    e_codes[n] = per_block.tile([P, SEEN, P], U32, name="e_codes", align_bytes=64)
+                    e_scales[n] = per_block.tile([P, SEEN, P], U8, name="e_scales", align_bytes=64)
+                nc.vector.quantize_mx(
+                    out=e_codes[n][:, w, :].bitcast(FP8X4),
+                    scales=e_scales[n][:, w, :],
+                    in_=grouped[n, w][:].rearrange("p q t -> p (q t)"),
+                )
 
         def product(n):
-            num_ps[n] = psum_num.tile([P, PACK, D], F32, name="num_ps")
+            num_ps[n] = psum_turns.tile([P, PACK, D], F32, name="num_ps", tag="turns")
             for r in range(PACK):
-                for side in range(first_side(n), 2):
-                    cols = slice(side * P, (side + 1) * P)
+                operands = []
+                if n > 0:
+                    operands.append((r, n - 1, v_codes[:, n - 1, :] if r == 0 else
+                                     v_part[:, n - 1, PACK - 2 + r, :]))
+                operands.append((r + 1, n, v_codes[:, n, :] if r == PACK - 1 else
+                                 v_part[:, n, r, :]))
+                for i, (w, m, codes) in enumerate(operands):
                     nc.tensor.matmul_mx(
                         out=num_ps[n][:, r, :],
-                        lhsT=e_codes[n][:, r, cols].bitcast(FP8X4),
-                        lhsT_scale=e_scales[n][:, r, cols],
-                        rhs=v_codes[:, n - 1 + side, :].bitcast(FP8X4),
-                        rhs_scale=v_scales[:, n - 1 + side, :],
-                        start=(side == first_side(n)),
-                        stop=(side == 1),
+                        lhsT=e_codes[n][:, w, :].bitcast(FP8X4),
+                        lhsT_scale=e_scales[n][:, w, :],
+                        rhs=codes.bitcast(FP8X4),
+                        rhs_scale=v_scales[:, m, :],
+                        start=(i == 0),
+                        stop=(i == len(operands) - 1),
                     )
 
         def row_sums(n):
@@ -249,13 +272,16 @@ def tile_exactslidingwindowattention_kernel(tc, q, k, v, out):
         def in_range(x, count):
             return 0 <= x < count
 
-        prepare_qk(0)
-        diagonal_scores(0)
-        diagonal_max(0)
-        for step in range(-1, TILES + 2 * PACK + 1):
+        prepare_k(0)
+        prepare_q(0)
+        for r in range(PACK):
+            diagonal_scores(0, r)
+        diagonal_max(0, 0, 1)
+        window_scores(1)
+        for step in range(TILES + PACK + 1):
             n, r = divmod(step, PACK)
-            if in_range(step + 1, TILES):
-                window_scores(step + 1)
+            if in_range(step + 2, TILES):
+                window_scores(step + 2)
             if in_range(step, TILES):
                 window_maximum(step)
             if in_range(step - 3, TILES):
@@ -263,23 +289,31 @@ def tile_exactslidingwindowattention_kernel(tc, q, k, v, out):
             if in_range(step, TILES):
                 row_maximum(step)
                 exponentials(step)
+            if step == 0:
+                diagonal_max(0, 1, PACK)
+                prepare_k(1)
+            if step == 1:
+                prepare_q(1)
             if in_range(step - 1, TILES):
                 transposed(step - 1)
-            if r == 0 and in_range(n + 1, BLOCKS):
-                prepare_qk(n + 1)
-            if r == 0 and in_range(n - 1, BLOCKS):
-                v_quantised(n - 1)
             if r == 0 and in_range(n - 2, BLOCKS):
                 normalised(n - 2)
-            if r == 1 and in_range(n + 1, BLOCKS):
-                diagonal_scores(n + 1)
+            if r == 1 and in_range(n + 2, BLOCKS):
+                prepare_k(n + 2)
+            if r == 1 and in_range(n, BLOCKS):
+                v_regrouped(n)
             if r == 1 and in_range(n - 1, BLOCKS):
                 row_sums(n - 1)
+            if r == 2 and in_range(n + 2, BLOCKS):
+                prepare_q(n + 2)
             if r == 2 and in_range(n + 1, BLOCKS):
-                diagonal_max(n + 1)
+                for i in range(PACK):
+                    diagonal_scores(n + 1, i)
+            if r == 2 and in_range(n, BLOCKS):
+                v_quantised(n)
             if r == 2 and in_range(n - 1, BLOCKS):
                 reciprocals(n - 1)
-            if r == 3 and in_range(n, BLOCKS):
-                v_regrouped(n)
+            if r == 3 and in_range(n + 1, BLOCKS):
+                diagonal_max(n + 1, 0, PACK)
             if r == 3 and in_range(n - 1, BLOCKS):
                 product(n - 1)

@@ -22,6 +22,7 @@ SLOT = P // PACK
 TILES = S // P
 BLOCKS = S // BLOCK
 SEEN = PACK + 1
+V_RING = 4
 SCALE = D ** -0.5
 MASKED = -3.0e38
 
@@ -52,9 +53,14 @@ def tile_exactslidingwindowattention_kernel(tc, q, k, v, out):
         for n in range(BLOCKS):
             nc.sync.dma_start(out=k_sb[:, n], in_=k_blocks[n])
             nc.sync.dma_start(out=q_sb[:, n], in_=q_blocks[n])
-            if n > 0:
-                nc.sync.dma_start(out=v_sb[:, n - 1], in_=v_blocks[n - 1])
-        nc.sync.dma_start(out=v_sb[:, BLOCKS - 1], in_=v_blocks[BLOCKS - 1])
+            nc.sync.dma_start(out=v_sb[:, n], in_=v_blocks[n])
+
+        variants = 2 * (PACK - 1)
+        v_part = []
+        for i in range(V_RING):
+            v_part_i = keep.tile([P, variants, D], U32, name="v_part%d" % i, align_bytes=64)
+            nc.vector.memset(v_part_i[:], 0)
+            v_part.append(v_part_i)
 
         ident = keep.tile([P, P], BF16)
         make_identity(nc, ident[:])
@@ -91,10 +97,6 @@ def tile_exactslidingwindowattention_kernel(tc, q, k, v, out):
         qT = keep.tile([D, S], BF16)
         v_codes = keep.tile([P, BLOCKS, D], U32, align_bytes=64)
         v_scales = keep.tile([P, BLOCKS, D], U8, align_bytes=64)
-        variants = 2 * (PACK - 1)
-        v_part = keep.tile([P, BLOCKS, variants, D], U32, align_bytes=64)
-        for n in range(BLOCKS):
-            nc.gpsimd.memset(v_part[:, n], 0)
 
         diag_ps = {}
         diag_max = {}
@@ -112,8 +114,8 @@ def tile_exactslidingwindowattention_kernel(tc, q, k, v, out):
         def earlier_tiles(T):
             return min(T, PACK)
 
-        def transposed_in(x_sb, n):
-            x_ps = psum_turns.tile([D, PACK, P], BF16, name="x_ps", tag="turns")
+        def transposed_in(x_sb, n, pool=psum_turns, tag="turns"):
+            x_ps = pool.tile([D, PACK, P], BF16, name="x_ps", tag=tag)
             for t in range(PACK):
                 nc.tensor.transpose(x_ps[:, t, :], x_sb[:, n, t, :], ident[:])
             return x_ps[:].rearrange("d t p -> d (t p)").bitcast(F32)
@@ -123,9 +125,11 @@ def tile_exactslidingwindowattention_kernel(tc, q, k, v, out):
                            in_=transposed_in(k_sb, n))
 
         def prepare_q(n):
-            copy = nc.vector.tensor_copy if n == 0 else nc.scalar.copy
-            copy(out=qT[:].bitcast(F32)[:, n * BLOCK // 2:(n + 1) * BLOCK // 2],
-                 in_=transposed_in(q_sb, n))
+            qT_n = qT[:].bitcast(F32)[:, n * BLOCK // 2:(n + 1) * BLOCK // 2]
+            if n == 0:
+                nc.vector.tensor_copy(out=qT_n, in_=transposed_in(q_sb, n, psum_eT, "eT_ps"))
+            else:
+                nc.scalar.copy(out=qT_n, in_=transposed_in(q_sb, n))
 
         def v_regrouped(n):
             v_grouped[n] = work.tile([P, D, PACK], BF16, name="v_grouped", align_bytes=64)
@@ -140,30 +144,35 @@ def tile_exactslidingwindowattention_kernel(tc, q, k, v, out):
             for s in range(PACK):
                 rows = slice(s * SLOT, (s + 1) * SLOT)
                 nc.sync.dma_start(
-                    out=v_part[rows, n, s:s + PACK - 1, :].bitcast(I32),
+                    out=v_part[n % V_RING][rows, s:s + PACK - 1, :].bitcast(I32),
                     in_=v_codes[rows, n, :].bitcast(I32).unsqueeze(1).to_broadcast(
                         [SLOT, PACK - 1, D]))
 
-        def diagonal_scores(n, r):
-            if r == 0:
-                diag_ps[n] = psum_diag.tile([P, PACK, P], F32, name="diag_ps")
-            T = n * PACK + r
-            nc.tensor.matmul(out=diag_ps[n][:, r, :], lhsT=qT[:, T * P:(T + 1) * P],
+        def own_tile_scores(T, out):
+            nc.tensor.matmul(out=out, lhsT=qT[:, T * P:(T + 1) * P],
                              rhs=kT[:, T * P:(T + 1) * P], start=True, stop=False)
-            nc.tensor.matmul(out=diag_ps[n][:, r, :], lhsT=ident[:], rhs=mask_own[:],
-                             start=False, stop=True)
+            nc.tensor.matmul(out=out, lhsT=ident[:], rhs=mask_own[:], start=False, stop=True)
 
-        def diagonal_max(n, r0, r1):
-            if r0 == 0:
-                diag_max[n] = small.tile([P, PACK], F32, name="diag_max")
-            nc.vector.tensor_reduce(out=diag_max[n][:, r0:r1], in_=diag_ps[n][:, r0:r1, :],
+        def first_diagonal(n):
+            return 1 if n == 0 else 0
+
+        def diagonal_scores(n):
+            diag_ps[n] = psum_diag.tile([P, PACK, P], F32, name="diag_ps")
+            for r in range(first_diagonal(n), PACK):
+                own_tile_scores(n * PACK + r, diag_ps[n][:, r, :])
+
+        def diagonal_max(n):
+            r0 = first_diagonal(n)
+            diag_max[n] = small.tile([P, PACK], F32, name="diag_max")
+            nc.vector.tensor_reduce(out=diag_max[n][:, r0:], in_=diag_ps[n][:, r0:, :],
                                     axis=AXIS.X, op=ALU.max)
 
         def window_scores(T):
             count = earlier_tiles(T)
-            if count == 0:
-                return
             window_ps[T] = psum_window.tile([P, BLOCK], F32, name="window_ps")
+            if T == 0:
+                own_tile_scores(T, window_ps[T][:, 0:P])
+                return
             clipped = count == PACK
             nc.tensor.matmul(out=window_ps[T][:, 0:count * P],
                              lhsT=qT[:, T * P:(T + 1) * P],
@@ -174,11 +183,10 @@ def tile_exactslidingwindowattention_kernel(tc, q, k, v, out):
                                  start=False, stop=True)
 
         def window_maximum(T):
-            if T > 0:
-                window_max[T] = small.tile([P, 1], F32, name="window_max")
-                nc.vector.tensor_reduce(out=window_max[T][:],
-                                        in_=window_ps[T][:, 0:earlier_tiles(T) * P],
-                                        axis=AXIS.X, op=ALU.max)
+            window_max[T] = small.tile([P, 1], F32, name="window_max")
+            nc.vector.tensor_reduce(out=window_max[T][:],
+                                    in_=window_ps[T][:, 0:max(earlier_tiles(T), 1) * P],
+                                    axis=AXIS.X, op=ALU.max)
 
         def row_maximum(T):
             n, r = divmod(T, PACK)
@@ -188,7 +196,7 @@ def tile_exactslidingwindowattention_kernel(tc, q, k, v, out):
                                         scalar1=diag_max[n][:, r:r + 1], scalar2=-SCALE,
                                         op0=ALU.max, op1=ALU.mult)
             else:
-                nc.vector.tensor_scalar(out=neg_max[T][:], in0=diag_max[n][:, r:r + 1],
+                nc.vector.tensor_scalar(out=neg_max[T][:], in0=window_max[T][:],
                                         scalar1=-SCALE, scalar2=None, op0=ALU.mult)
 
         def exponentials(T):
@@ -201,7 +209,8 @@ def tile_exactslidingwindowattention_kernel(tc, q, k, v, out):
                     in_=window_ps[T][:, 0:count * P],
                     func=ACT.Exp, bias=neg_max[T][:], scale=SCALE,
                     accum_out=den_parts[:, n, r, 0:1])
-            nc.scalar.activation(out=e_row[n][:, own, :], in_=diag_ps[n][:, r, :],
+            nc.scalar.activation(out=e_row[n][:, own, :],
+                                 in_=diag_ps[n][:, r, :] if T > 0 else window_ps[T][:, 0:P],
                                  func=ACT.Exp, bias=neg_max[T][:], scale=SCALE,
                                  accum_out=den_parts[:, n, r, 1:2])
 
@@ -240,9 +249,9 @@ def tile_exactslidingwindowattention_kernel(tc, q, k, v, out):
                 operands = []
                 if n > 0:
                     operands.append((r, n - 1, v_codes[:, n - 1, :] if r == 0 else
-                                     v_part[:, n - 1, PACK - 2 + r, :]))
+                                     v_part[(n - 1) % V_RING][:, PACK - 2 + r, :]))
                 operands.append((r + 1, n, v_codes[:, n, :] if r == PACK - 1 else
-                                 v_part[:, n, r, :]))
+                                 v_part[n % V_RING][:, r, :]))
                 for i, (w, m, codes) in enumerate(operands):
                     nc.tensor.matmul_mx(
                         out=num_ps[n][:, r, :],
@@ -274,10 +283,9 @@ def tile_exactslidingwindowattention_kernel(tc, q, k, v, out):
 
         prepare_k(0)
         prepare_q(0)
-        for r in range(PACK):
-            diagonal_scores(0, r)
-        diagonal_max(0, 0, 1)
+        window_scores(0)
         window_scores(1)
+        diagonal_scores(0)
         for step in range(TILES + PACK + 1):
             n, r = divmod(step, PACK)
             if in_range(step + 2, TILES):
@@ -290,9 +298,11 @@ def tile_exactslidingwindowattention_kernel(tc, q, k, v, out):
                 row_maximum(step)
                 exponentials(step)
             if step == 0:
-                diagonal_max(0, 1, PACK)
+                diagonal_max(0)
+                v_regrouped(0)
                 prepare_k(1)
             if step == 1:
+                v_quantised(0)
                 prepare_q(1)
             if in_range(step - 1, TILES):
                 transposed(step - 1)
@@ -300,20 +310,19 @@ def tile_exactslidingwindowattention_kernel(tc, q, k, v, out):
                 normalised(n - 2)
             if r == 1 and in_range(n + 2, BLOCKS):
                 prepare_k(n + 2)
-            if r == 1 and in_range(n, BLOCKS):
-                v_regrouped(n)
+            if r == 1 and in_range(n + 1, BLOCKS):
+                v_regrouped(n + 1)
             if r == 1 and in_range(n - 1, BLOCKS):
                 row_sums(n - 1)
             if r == 2 and in_range(n + 2, BLOCKS):
                 prepare_q(n + 2)
             if r == 2 and in_range(n + 1, BLOCKS):
-                for i in range(PACK):
-                    diagonal_scores(n + 1, i)
-            if r == 2 and in_range(n, BLOCKS):
-                v_quantised(n)
+                diagonal_scores(n + 1)
+            if r == 2 and in_range(n + 1, BLOCKS):
+                v_quantised(n + 1)
             if r == 2 and in_range(n - 1, BLOCKS):
                 reciprocals(n - 1)
             if r == 3 and in_range(n + 1, BLOCKS):
-                diagonal_max(n + 1, 0, PACK)
+                diagonal_max(n + 1)
             if r == 3 and in_range(n - 1, BLOCKS):
                 product(n - 1)

@@ -64,34 +64,29 @@ def tile_exactslidingwindowattention_kernel(tc, q, k, v, out):
 
         ident = keep.tile([P, P], BF16)
         make_identity(nc, ident[:])
-        ident_f32 = keep.tile([P, P], F32)
-        make_identity(nc, ident_f32[:])
-        mask_own_f32 = keep.tile([P, P], F32)
-        nc.gpsimd.memset(mask_own_f32[:], 0.0)
+        mask_own = keep.tile([P, P], BF16)
+        nc.gpsimd.memset(mask_own[:], 0.0)
         nc.gpsimd.affine_select(
-            out=mask_own_f32[:], in_=mask_own_f32[:], compare_op=ALU.is_ge, fill=MASKED,
+            out=mask_own[:], in_=mask_own[:], compare_op=ALU.is_ge, fill=MASKED,
             base=0, pattern=[[-1, P]], channel_multiplier=1,
         )
-        mask_prev_f32 = keep.tile([P, P], F32)
-        nc.gpsimd.memset(mask_prev_f32[:], 0.0)
+        mask_prev = keep.tile([P, P], BF16)
+        nc.gpsimd.memset(mask_prev[:], 0.0)
         nc.gpsimd.affine_select(
-            out=mask_prev_f32[:], in_=mask_prev_f32[:], compare_op=ALU.is_ge, fill=MASKED,
+            out=mask_prev[:], in_=mask_prev[:], compare_op=ALU.is_ge, fill=MASKED,
             base=-1, pattern=[[1, P]], channel_multiplier=-1,
         )
-
-        mask_own = keep.tile([P, P], BF16)
-        nc.vector.tensor_copy(out=mask_own[:], in_=mask_own_f32[:])
-        mask_prev = keep.tile([P, P], BF16)
-        nc.vector.tensor_copy(out=mask_prev[:], in_=mask_prev_f32[:])
+        ident_f32 = keep.tile([P, P], F32)
+        make_identity(nc, ident_f32[:])
 
         e_row = []
         for n in range(BLOCKS):
             e_row_n = keep.tile([P, PACK * SEEN, P], BF16, name="e_row%d" % n)
             e_row.append(e_row_n)
         for r in range(1, PACK):
-            nc.vector.memset(e_row[0][:, SEEN * r:SEEN * r + PACK - r, :], 0.0)
+            nc.gpsimd.memset(e_row[0][:, SEEN * r:SEEN * r + PACK - r, :], 0.0)
         den_parts = keep.tile([P, BLOCKS, PACK, 2], F32)
-        nc.vector.memset(den_parts[:], 0.0)
+        nc.gpsimd.memset(den_parts[:], 0.0)
 
         kT = keep.tile([D, S], BF16)
         qT = keep.tile([D, S], BF16)
@@ -156,9 +151,10 @@ def tile_exactslidingwindowattention_kernel(tc, q, k, v, out):
         def first_diagonal(n):
             return 1 if n == 0 else 0
 
-        def diagonal_scores(n):
-            diag_ps[n] = psum_diag.tile([P, PACK, P], F32, name="diag_ps")
-            for r in range(first_diagonal(n), PACK):
+        def diagonal_scores(n, tiles):
+            if n not in diag_ps:
+                diag_ps[n] = psum_diag.tile([P, PACK, P], F32, name="diag_ps")
+            for r in tiles:
                 own_tile_scores(n * PACK + r, diag_ps[n][:, r, :])
 
         def diagonal_max(n):
@@ -199,7 +195,7 @@ def tile_exactslidingwindowattention_kernel(tc, q, k, v, out):
                 nc.vector.tensor_scalar(out=neg_max[T][:], in0=window_max[T][:],
                                         scalar1=-SCALE, scalar2=None, op0=ALU.mult)
 
-        def exponentials(T):
+        def window_exponentials(T):
             n, r = divmod(T, PACK)
             count = earlier_tiles(T)
             own = SEEN * r + PACK
@@ -209,43 +205,47 @@ def tile_exactslidingwindowattention_kernel(tc, q, k, v, out):
                     in_=window_ps[T][:, 0:count * P],
                     func=ACT.Exp, bias=neg_max[T][:], scale=SCALE,
                     accum_out=den_parts[:, n, r, 0:1])
-            nc.scalar.activation(out=e_row[n][:, own, :],
+
+        def own_tile_exponentials(T):
+            n, r = divmod(T, PACK)
+            nc.scalar.activation(out=e_row[n][:, SEEN * r + PACK, :],
                                  in_=diag_ps[n][:, r, :] if T > 0 else window_ps[T][:, 0:P],
                                  func=ACT.Exp, bias=neg_max[T][:], scale=SCALE,
                                  accum_out=den_parts[:, n, r, 1:2])
 
         def units(T):
             n, r = divmod(T, PACK)
-            done = range((SEEN * r) // PACK, (SEEN * (r + 1)) // PACK)
+            done = range((SEEN * r) // PACK, (SEEN * (r + 1)) // PACK) if T >= 0 else ()
             return [(n, w) for w in done if n > 0 or w > 0]
 
-        def transposed(T):
-            for n, w in units(T):
-                eT_ps = psum_eT.tile([P, 2, P], F32, name="eT_ps")
-                words = e_row[n][:].rearrange("p a c -> p (a c)").bitcast(F32)
-                for u in range(2):
-                    nc.tensor.transpose(eT_ps[:, u, :], words[:, 2 * w * P + u:2 * (w + 1) * P:2],
-                                        ident_f32[:])
-                grouped[n, w] = work.tile([P, P, PACK], BF16, name="grouped", align_bytes=64)
-                nc.scalar.copy(
-                    out=grouped[n, w][:].rearrange("p q t -> p (q t)").bitcast(F32).rearrange(
-                        "p (q u) -> p q u", u=2),
-                    in_=eT_ps[:].rearrange("p u q -> p q u"))
+        def transposed(n, w, copy):
+            eT_ps = psum_eT.tile([P, 2, P], F32, name="eT_ps")
+            words = e_row[n][:].rearrange("p a c -> p (a c)").bitcast(F32)
+            for u in range(2):
+                nc.tensor.transpose(eT_ps[:, u, :], words[:, 2 * w * P + u:2 * (w + 1) * P:2],
+                                    ident_f32[:])
+            grouped[n, w] = work.tile([P, P, PACK], BF16, name="grouped", align_bytes=64)
+            copy(
+                out=grouped[n, w][:].rearrange("p q t -> p (q t)").bitcast(F32).rearrange(
+                    "p (q u) -> p q u", u=2),
+                in_=eT_ps[:].rearrange("p u q -> p q u"))
 
-        def quantised(T):
-            for n, w in units(T):
-                if w == (1 if n == 0 else 0):
-                    e_codes[n] = per_block.tile([P, SEEN, P], U32, name="e_codes", align_bytes=64)
-                    e_scales[n] = per_block.tile([P, SEEN, P], U8, name="e_scales", align_bytes=64)
-                nc.vector.quantize_mx(
-                    out=e_codes[n][:, w, :].bitcast(FP8X4),
-                    scales=e_scales[n][:, w, :],
-                    in_=grouped[n, w][:].rearrange("p q t -> p (q t)"),
-                )
+        def quantised(n, w):
+            if w == (1 if n == 0 else 0):
+                e_codes[n] = per_block.tile([P, SEEN, P], U32, name="e_codes", align_bytes=64)
+                e_scales[n] = per_block.tile([P, SEEN, P], U8, name="e_scales", align_bytes=64)
+            nc.vector.quantize_mx(
+                out=e_codes[n][:, w, :].bitcast(FP8X4),
+                scales=e_scales[n][:, w, :],
+                in_=grouped[n, w][:].rearrange("p q t -> p (q t)"),
+            )
 
-        def product(n):
-            num_ps[n] = psum_turns.tile([P, PACK, D], F32, name="num_ps", tag="turns")
-            for r in range(PACK):
+        def product(n, tiles):
+            if n < BLOCKS - 1:
+                num_ps[n] = psum_turns.tile([P, PACK, D], F32, name="num_ps", tag="turns")
+            else:
+                num_ps[n] = psum_window.tile([P, PACK, D], F32, name="num_ps", tag="window_ps")
+            for r in tiles:
                 operands = []
                 if n > 0:
                     operands.append((r, n - 1, v_codes[:, n - 1, :] if r == 0 else
@@ -271,12 +271,12 @@ def tile_exactslidingwindowattention_kernel(tc, q, k, v, out):
             inv_den[n] = small.tile([P, PACK], F32, name="inv_den")
             nc.vector.reciprocal(out=inv_den[n][:], in_=den[n][:])
 
-        def normalised(n):
-            out_sb = per_block.tile([P, PACK, D], F32)
-            nc.vector.tensor_tensor(out=out_sb[:], in0=num_ps[n][:],
-                                    in1=inv_den[n][:].unsqueeze(2).to_broadcast([P, PACK, D]),
-                                    op=ALU.mult)
-            nc.sync.dma_start(out=out_blocks[n], in_=out_sb[:])
+        def normalised(n, r0=0, r1=PACK):
+            out_sb = work.tile([P, PACK, D], F32, name="out_sb")
+            nc.vector.tensor_tensor(
+                out=out_sb[:, r0:r1, :], in0=num_ps[n][:, r0:r1, :],
+                in1=inv_den[n][:, r0:r1].unsqueeze(2).to_broadcast([P, r1 - r0, D]), op=ALU.mult)
+            nc.sync.dma_start(out=out_blocks[n][:, r0:r1, :], in_=out_sb[:, r0:r1, :])
 
         def in_range(x, count):
             return 0 <= x < count
@@ -285,18 +285,17 @@ def tile_exactslidingwindowattention_kernel(tc, q, k, v, out):
         prepare_q(0)
         window_scores(0)
         window_scores(1)
-        diagonal_scores(0)
-        for step in range(TILES + PACK + 1):
+        diagonal_scores(0, range(first_diagonal(0), PACK))
+        for step in range(TILES):
             n, r = divmod(step, PACK)
-            if in_range(step + 2, TILES):
+            if step + 2 < TILES:
                 window_scores(step + 2)
-            if in_range(step, TILES):
-                window_maximum(step)
-            if in_range(step - 3, TILES):
-                quantised(step - 3)
-            if in_range(step, TILES):
-                row_maximum(step)
-                exponentials(step)
+            window_maximum(step)
+            for unit in units(step - 3):
+                quantised(*unit)
+            row_maximum(step)
+            window_exponentials(step)
+            own_tile_exponentials(step)
             if step == 0:
                 diagonal_max(0)
                 v_regrouped(0)
@@ -304,25 +303,42 @@ def tile_exactslidingwindowattention_kernel(tc, q, k, v, out):
             if step == 1:
                 v_quantised(0)
                 prepare_q(1)
-            if in_range(step - 1, TILES):
-                transposed(step - 1)
-            if r == 0 and in_range(n - 2, BLOCKS):
+            for unit in units(step - 1):
+                transposed(*unit, nc.scalar.copy)
+            if r == 0 and n >= 2:
                 normalised(n - 2)
-            if r == 1 and in_range(n + 2, BLOCKS):
+            if r == 1 and n + 2 < BLOCKS:
                 prepare_k(n + 2)
-            if r == 1 and in_range(n + 1, BLOCKS):
+            if r == 1 and n + 1 < BLOCKS:
                 v_regrouped(n + 1)
-            if r == 1 and in_range(n - 1, BLOCKS):
+            if r == 1 and n >= 1:
                 row_sums(n - 1)
-            if r == 2 and in_range(n + 2, BLOCKS):
+            if r == 2 and n + 2 < BLOCKS:
                 prepare_q(n + 2)
-            if r == 2 and in_range(n + 1, BLOCKS):
-                diagonal_scores(n + 1)
-            if r == 2 and in_range(n + 1, BLOCKS):
+            if r < 3 and n + 1 < BLOCKS:
+                shares = ([], [0, 1], [2, 3]) if n == 0 else ([0, 1], [2], [3])
+                diagonal_scores(n + 1, shares[r])
+            if r == 2 and n + 1 < BLOCKS:
                 v_quantised(n + 1)
-            if r == 2 and in_range(n - 1, BLOCKS):
+            if r == 2 and n >= 1:
                 reciprocals(n - 1)
-            if r == 3 and in_range(n + 1, BLOCKS):
+            if r == 3 and n + 1 < BLOCKS:
                 diagonal_max(n + 1)
-            if r == 3 and in_range(n - 1, BLOCKS):
-                product(n - 1)
+            if r == 3 and n >= 1:
+                product(n - 1, range(PACK))
+
+        last = BLOCKS - 1
+        w_before, w_last = 3, 4
+        transposed(last, w_before, nc.scalar.copy)
+        quantised(last, 1)
+        row_sums(last)
+        normalised(last - 1)
+        quantised(last, 2)
+        reciprocals(last)
+        transposed(last, w_last, nc.vector.tensor_copy)
+        product(last, range(0, 2))
+        quantised(last, w_before)
+        quantised(last, w_last)
+        normalised(last, 0, 2)
+        product(last, range(2, PACK))
+        normalised(last, 2, PACK)

@@ -21,7 +21,9 @@ BLOCK = PACK * P
 SLOT = P // PACK
 TILES = S // P
 BLOCKS = S // BLOCK
-SEEN = PACK + 1
+HALF = P // 2
+OWN = PACK
+V_ROW = D + D // 4
 V_RING = 4
 SCALE = D ** -0.5
 MASKED = -3.0e38
@@ -43,9 +45,9 @@ def tile_exactslidingwindowattention_kernel(tc, q, k, v, out):
         per_block = ctx.enter_context(tc.tile_pool(name="per_block", bufs=2))
         small = ctx.enter_context(tc.tile_pool(name="small", bufs=4))
         psum_window = ctx.enter_context(tc.psum_pool(name="psum_window", bufs=3))
-        psum_diag = ctx.enter_context(tc.psum_pool(name="psum_diag", bufs=2))
-        psum_eT = ctx.enter_context(tc.psum_pool(name="psum_eT", bufs=2))
-        psum_turns = ctx.enter_context(tc.psum_pool(name="psum_turns", bufs=1))
+        psum_own = ctx.enter_context(tc.psum_pool(name="psum_own", bufs=2))
+        psum_turns = ctx.enter_context(tc.psum_pool(name="psum_turns", bufs=2))
+        psum_num = ctx.enter_context(tc.psum_pool(name="psum_num", bufs=1))
 
         q_sb = keep.tile([P, BLOCKS, PACK, D], BF16)
         k_sb = keep.tile([P, BLOCKS, PACK, D], BF16)
@@ -55,12 +57,14 @@ def tile_exactslidingwindowattention_kernel(tc, q, k, v, out):
             nc.sync.dma_start(out=q_sb[:, n], in_=q_blocks[n])
             nc.sync.dma_start(out=v_sb[:, n], in_=v_blocks[n])
 
-        variants = 2 * (PACK - 1)
-        v_part = []
+        kT = keep.tile([D, S], BF16)
+        qT = keep.tile([D, S], BF16)
+        v_mx = keep.tile([P, BLOCKS, V_ROW], U32, align_bytes=64)
+        v_slot = []
         for i in range(V_RING):
-            v_part_i = keep.tile([P, variants, D], U32, name="v_part%d" % i, align_bytes=64)
-            nc.vector.memset(v_part_i[:], 0)
-            v_part.append(v_part_i)
+            v_slot_i = keep.tile([P, PACK, D], U32, name="v_slot%d" % i, align_bytes=64)
+            nc.vector.memset(v_slot_i[:], 0)
+            v_slot.append(v_slot_i)
 
         ident = keep.tile([P, P], BF16)
         make_identity(nc, ident[:])
@@ -79,38 +83,34 @@ def tile_exactslidingwindowattention_kernel(tc, q, k, v, out):
         ident_f32 = keep.tile([P, P], F32)
         make_identity(nc, ident_f32[:])
 
-        e_row = []
-        for n in range(BLOCKS):
-            e_row_n = keep.tile([P, PACK * SEEN, P], BF16, name="e_row%d" % n)
-            e_row.append(e_row_n)
-        for r in range(1, PACK):
-            nc.gpsimd.memset(e_row[0][:, SEEN * r:SEEN * r + PACK - r, :], 0.0)
+        nc.gpsimd.memset(v_mx[:, :, D:], 0)
+        e_first = {}
+        for T in range(1, PACK):
+            e_first[T] = keep.tile([P, 2, PACK * HALF], BF16, name="e_first%d" % T)
+            nc.gpsimd.memset(e_first[T][:], 0.0)
         den_parts = keep.tile([P, BLOCKS, PACK, 2], F32)
         nc.gpsimd.memset(den_parts[:], 0.0)
 
-        kT = keep.tile([D, S], BF16)
-        qT = keep.tile([D, S], BF16)
-        v_codes = keep.tile([P, BLOCKS, D], U32, align_bytes=64)
-        v_scales = keep.tile([P, BLOCKS, D], U8, align_bytes=64)
-
-        diag_ps = {}
-        diag_max = {}
+        own_ps = {}
+        own_max = {}
         window_ps = {}
         window_max = {}
         neg_max = {}
         v_grouped = {}
+        v_window = {}
         den = {}
         inv_den = {}
         num_ps = {}
+        e_unit = {}
         grouped = {}
         e_codes = {}
         e_scales = {}
 
-        def earlier_tiles(T):
+        def window_tiles(T):
             return min(T, PACK)
 
-        def transposed_in(x_sb, n, pool=psum_turns, tag="turns"):
-            x_ps = pool.tile([D, PACK, P], BF16, name="x_ps", tag=tag)
+        def transposed_in(x_sb, n):
+            x_ps = psum_turns.tile([D, PACK, P], BF16, name="x_ps", tag="turns")
             for t in range(PACK):
                 nc.tensor.transpose(x_ps[:, t, :], x_sb[:, n, t, :], ident[:])
             return x_ps[:].rearrange("d t p -> d (t p)").bitcast(F32)
@@ -122,7 +122,7 @@ def tile_exactslidingwindowattention_kernel(tc, q, k, v, out):
         def prepare_q(n):
             qT_n = qT[:].bitcast(F32)[:, n * BLOCK // 2:(n + 1) * BLOCK // 2]
             if n == 0:
-                nc.vector.tensor_copy(out=qT_n, in_=transposed_in(q_sb, n, psum_eT, "eT_ps"))
+                nc.vector.tensor_copy(out=qT_n, in_=transposed_in(q_sb, n))
             else:
                 nc.scalar.copy(out=qT_n, in_=transposed_in(q_sb, n))
 
@@ -130,41 +130,54 @@ def tile_exactslidingwindowattention_kernel(tc, q, k, v, out):
             v_grouped[n] = work.tile([P, D, PACK], BF16, name="v_grouped", align_bytes=64)
             nc.vector.tensor_copy(out=v_grouped[n][:], in_=v_sb[:, n].rearrange("p t d -> p d t"))
 
+        def v_scales(row):
+            return row[:, D:].bitcast(U8)
+
         def v_quantised(n):
             nc.vector.quantize_mx(
-                out=v_codes[:, n, :].bitcast(FP8X4),
-                scales=v_scales[:, n, :],
+                out=v_mx[:, n, 0:D].bitcast(FP8X4),
+                scales=v_scales(v_mx[:, n]),
                 in_=v_grouped[n][:].rearrange("p d t -> p (d t)"),
             )
+
+        def v_rearranged(n):
             for s in range(PACK):
                 rows = slice(s * SLOT, (s + 1) * SLOT)
-                nc.sync.dma_start(
-                    out=v_part[n % V_RING][rows, s:s + PACK - 1, :].bitcast(I32),
-                    in_=v_codes[rows, n, :].bitcast(I32).unsqueeze(1).to_broadcast(
-                        [SLOT, PACK - 1, D]))
+                nc.sync.dma_start(out=v_slot[n % V_RING][rows, s, :].bitcast(I32),
+                                  in_=v_mx[rows, n, 0:D].bitcast(I32))
+            if n == 0:
+                return
+            v_window[n] = work.tile([P, PACK - 1, V_ROW], U32, name="v_window",
+                                    align_bytes=64)
+            for r in range(1, PACK):
+                cut = (PACK - r) * SLOT
+                nc.sync.dma_start(out=v_window[n][0:cut, r - 1, :].bitcast(I32),
+                                  in_=v_mx[P - cut:P, n - 1, :].bitcast(I32))
+                nc.sync.dma_start(out=v_window[n][cut:P, r - 1, :].bitcast(I32),
+                                  in_=v_mx[0:P - cut, n, :].bitcast(I32))
 
         def own_tile_scores(T, out):
             nc.tensor.matmul(out=out, lhsT=qT[:, T * P:(T + 1) * P],
                              rhs=kT[:, T * P:(T + 1) * P], start=True, stop=False)
             nc.tensor.matmul(out=out, lhsT=ident[:], rhs=mask_own[:], start=False, stop=True)
 
-        def first_diagonal(n):
+        def first_own(n):
             return 1 if n == 0 else 0
 
-        def diagonal_scores(n, tiles):
-            if n not in diag_ps:
-                diag_ps[n] = psum_diag.tile([P, PACK, P], F32, name="diag_ps")
+        def own_scores(n, tiles):
+            if n not in own_ps:
+                own_ps[n] = psum_own.tile([P, PACK, P], F32, name="own_ps")
             for r in tiles:
-                own_tile_scores(n * PACK + r, diag_ps[n][:, r, :])
+                own_tile_scores(n * PACK + r, own_ps[n][:, r, :])
 
-        def diagonal_max(n):
-            r0 = first_diagonal(n)
-            diag_max[n] = small.tile([P, PACK], F32, name="diag_max")
-            nc.vector.tensor_reduce(out=diag_max[n][:, r0:], in_=diag_ps[n][:, r0:, :],
+        def own_maximum(n):
+            r0 = first_own(n)
+            own_max[n] = small.tile([P, PACK], F32, name="own_max")
+            nc.vector.tensor_reduce(out=own_max[n][:, r0:], in_=own_ps[n][:, r0:, :],
                                     axis=AXIS.X, op=ALU.max)
 
         def window_scores(T):
-            count = earlier_tiles(T)
+            count = window_tiles(T)
             window_ps[T] = psum_window.tile([P, BLOCK], F32, name="window_ps")
             if T == 0:
                 own_tile_scores(T, window_ps[T][:, 0:P])
@@ -181,7 +194,7 @@ def tile_exactslidingwindowattention_kernel(tc, q, k, v, out):
         def window_maximum(T):
             window_max[T] = small.tile([P, 1], F32, name="window_max")
             nc.vector.tensor_reduce(out=window_max[T][:],
-                                    in_=window_ps[T][:, 0:max(earlier_tiles(T), 1) * P],
+                                    in_=window_ps[T][:, 0:max(window_tiles(T), 1) * P],
                                     axis=AXIS.X, op=ALU.max)
 
         def row_maximum(T):
@@ -189,41 +202,44 @@ def tile_exactslidingwindowattention_kernel(tc, q, k, v, out):
             neg_max[T] = small.tile([P, 1], F32, name="neg_max")
             if T > 0:
                 nc.vector.tensor_scalar(out=neg_max[T][:], in0=window_max[T][:],
-                                        scalar1=diag_max[n][:, r:r + 1], scalar2=-SCALE,
+                                        scalar1=own_max[n][:, r:r + 1], scalar2=-SCALE,
                                         op0=ALU.max, op1=ALU.mult)
             else:
                 nc.vector.tensor_scalar(out=neg_max[T][:], in0=window_max[T][:],
                                         scalar1=-SCALE, scalar2=None, op0=ALU.mult)
 
+        def exponentials(T, scores, e_out, part):
+            n, r = divmod(T, PACK)
+            nc.scalar.activation(out=e_out.rearrange("p u (w e) -> p u w e", e=2),
+                                 in_=scores.rearrange("p (w u e) -> p u w e", u=2, e=2),
+                                 func=ACT.Exp, bias=neg_max[T][:], scale=SCALE,
+                                 accum_out=den_parts[:, n, r, part:part + 1])
+
         def window_exponentials(T):
             n, r = divmod(T, PACK)
-            count = earlier_tiles(T)
-            own = SEEN * r + PACK
-            if T > 0:
-                nc.scalar.activation(
-                    out=e_row[n][:, own - count:own, :].rearrange("p a c -> p (a c)"),
-                    in_=window_ps[T][:, 0:count * P],
-                    func=ACT.Exp, bias=neg_max[T][:], scale=SCALE,
-                    accum_out=den_parts[:, n, r, 0:1])
+            if T == 0:
+                return
+            count = window_tiles(T)
+            e_unit[n, r] = e_first[T] if T in e_first else work.tile(
+                [P, 2, PACK * HALF], BF16, name="e_window")
+            exponentials(T, window_ps[T][:, 0:count * P], e_unit[n, r][:, :, 0:count * HALF], 0)
 
-        def own_tile_exponentials(T):
+        def own_exponentials(T):
             n, r = divmod(T, PACK)
-            nc.scalar.activation(out=e_row[n][:, SEEN * r + PACK, :],
-                                 in_=diag_ps[n][:, r, :] if T > 0 else window_ps[T][:, 0:P],
-                                 func=ACT.Exp, bias=neg_max[T][:], scale=SCALE,
-                                 accum_out=den_parts[:, n, r, 1:2])
+            if r == 0:
+                e_unit[n, OWN] = per_block.tile([P, 2, PACK * HALF], BF16, name="e_own")
+            exponentials(T, own_ps[n][:, r, :] if T > 0 else window_ps[T][:, 0:P],
+                         e_unit[n, OWN][:, :, r * HALF:(r + 1) * HALF], 1)
 
         def units(T):
             n, r = divmod(T, PACK)
-            done = range((SEEN * r) // PACK, (SEEN * (r + 1)) // PACK) if T >= 0 else ()
-            return [(n, w) for w in done if n > 0 or w > 0]
+            return ([(n, r)] if T > 0 else []) + ([(n, OWN)] if r == PACK - 1 and T > 0 else [])
 
         def transposed(n, w, copy):
-            eT_ps = psum_eT.tile([P, 2, P], F32, name="eT_ps")
-            words = e_row[n][:].rearrange("p a c -> p (a c)").bitcast(F32)
+            eT_ps = psum_turns.tile([P, 2, P], F32, name="eT_ps", tag="turns")
+            words = e_unit[n, w][:].rearrange("p u c -> p (u c)").bitcast(F32)
             for u in range(2):
-                nc.tensor.transpose(eT_ps[:, u, :], words[:, 2 * w * P + u:2 * (w + 1) * P:2],
-                                    ident_f32[:])
+                nc.tensor.transpose(eT_ps[:, u, :], words[:, u * P:(u + 1) * P], ident_f32[:])
             grouped[n, w] = work.tile([P, P, PACK], BF16, name="grouped", align_bytes=64)
             copy(
                 out=grouped[n, w][:].rearrange("p q t -> p (q t)").bitcast(F32).rearrange(
@@ -231,9 +247,9 @@ def tile_exactslidingwindowattention_kernel(tc, q, k, v, out):
                 in_=eT_ps[:].rearrange("p u q -> p q u"))
 
         def quantised(n, w):
-            if w == (1 if n == 0 else 0):
-                e_codes[n] = per_block.tile([P, SEEN, P], U32, name="e_codes", align_bytes=64)
-                e_scales[n] = per_block.tile([P, SEEN, P], U8, name="e_scales", align_bytes=64)
+            if n not in e_codes:
+                e_codes[n] = per_block.tile([P, PACK + 1, P], U32, name="e_codes", align_bytes=64)
+                e_scales[n] = per_block.tile([P, PACK + 1, P], U8, name="e_scales", align_bytes=64)
             nc.vector.quantize_mx(
                 out=e_codes[n][:, w, :].bitcast(FP8X4),
                 scales=e_scales[n][:, w, :],
@@ -242,23 +258,24 @@ def tile_exactslidingwindowattention_kernel(tc, q, k, v, out):
 
         def product(n, tiles):
             if n < BLOCKS - 1:
-                num_ps[n] = psum_turns.tile([P, PACK, D], F32, name="num_ps", tag="turns")
+                sums = psum_num.tile([P, PACK, D], F32, name="num_ps")
             else:
-                num_ps[n] = psum_window.tile([P, PACK, D], F32, name="num_ps", tag="window_ps")
+                sums = psum_window.tile([P, PACK, D], F32, name="num_ps", tag="window_ps")
             for r in tiles:
-                operands = []
+                num_ps[n, r] = sums
+                operands = [(OWN, v_slot[n % V_RING][:, r, :], v_scales(v_mx[:, n]))]
+                if n == 0 and r > 0:
+                    operands.append((r, v_mx[:, 0, 0:D], v_scales(v_mx[:, 0])))
                 if n > 0:
-                    operands.append((r, n - 1, v_codes[:, n - 1, :] if r == 0 else
-                                     v_part[(n - 1) % V_RING][:, PACK - 2 + r, :]))
-                operands.append((r + 1, n, v_codes[:, n, :] if r == PACK - 1 else
-                                 v_part[n % V_RING][:, r, :]))
-                for i, (w, m, codes) in enumerate(operands):
+                    row = v_mx[:, n - 1] if r == 0 else v_window[n][:, r - 1]
+                    operands.append((r, row[:, 0:D], v_scales(row)))
+                for i, (w, codes, scales) in enumerate(operands):
                     nc.tensor.matmul_mx(
-                        out=num_ps[n][:, r, :],
+                        out=sums[:, r, :],
                         lhsT=e_codes[n][:, w, :].bitcast(FP8X4),
                         lhsT_scale=e_scales[n][:, w, :],
                         rhs=codes.bitcast(FP8X4),
-                        rhs_scale=v_scales[:, m, :],
+                        rhs_scale=scales,
                         start=(i == 0),
                         stop=(i == len(operands) - 1),
                     )
@@ -274,18 +291,15 @@ def tile_exactslidingwindowattention_kernel(tc, q, k, v, out):
         def normalised(n, r0=0, r1=PACK):
             out_sb = work.tile([P, PACK, D], F32, name="out_sb")
             nc.vector.tensor_tensor(
-                out=out_sb[:, r0:r1, :], in0=num_ps[n][:, r0:r1, :],
+                out=out_sb[:, r0:r1, :], in0=num_ps[n, r0][:, r0:r1, :],
                 in1=inv_den[n][:, r0:r1].unsqueeze(2).to_broadcast([P, r1 - r0, D]), op=ALU.mult)
             nc.sync.dma_start(out=out_blocks[n][:, r0:r1, :], in_=out_sb[:, r0:r1, :])
-
-        def in_range(x, count):
-            return 0 <= x < count
 
         prepare_k(0)
         prepare_q(0)
         window_scores(0)
         window_scores(1)
-        diagonal_scores(0, range(first_diagonal(0), PACK))
+        own_scores(0, range(first_own(0), PACK))
         for step in range(TILES):
             n, r = divmod(step, PACK)
             if step + 2 < TILES:
@@ -294,51 +308,59 @@ def tile_exactslidingwindowattention_kernel(tc, q, k, v, out):
             for unit in units(step - 3):
                 quantised(*unit)
             row_maximum(step)
-            window_exponentials(step)
-            own_tile_exponentials(step)
+            if step == TILES - 1:
+                own_exponentials(step)
+                window_exponentials(step)
+            else:
+                window_exponentials(step)
+                own_exponentials(step)
             if step == 0:
-                diagonal_max(0)
+                own_maximum(0)
                 v_regrouped(0)
                 prepare_k(1)
             if step == 1:
                 v_quantised(0)
+                v_rearranged(0)
                 prepare_q(1)
-            for unit in units(step - 1):
-                transposed(*unit, nc.scalar.copy)
-            if r == 0 and n >= 2:
+            if step < TILES - 1:
+                for unit in units(step - 1):
+                    transposed(*unit, nc.scalar.copy)
+            if r == 1 and n >= 2:
                 normalised(n - 2)
             if r == 1 and n + 2 < BLOCKS:
                 prepare_k(n + 2)
-            if r == 1 and n + 1 < BLOCKS:
+            if r == 0 and n + 1 < BLOCKS:
                 v_regrouped(n + 1)
             if r == 1 and n >= 1:
                 row_sums(n - 1)
             if r == 2 and n + 2 < BLOCKS:
                 prepare_q(n + 2)
             if r < 3 and n + 1 < BLOCKS:
-                shares = ([], [0, 1], [2, 3]) if n == 0 else ([0, 1], [2], [3])
-                diagonal_scores(n + 1, shares[r])
+                shares = ([], [0, 1], [2, 3]) if n == 0 else ([0, 1], [2, 3], [])
+                own_scores(n + 1, shares[r])
             if r == 2 and n + 1 < BLOCKS:
                 v_quantised(n + 1)
+                v_rearranged(n + 1)
             if r == 2 and n >= 1:
                 reciprocals(n - 1)
             if r == 3 and n + 1 < BLOCKS:
-                diagonal_max(n + 1)
-            if r == 3 and n >= 1:
+                own_maximum(n + 1)
+            if r == 3 and n >= 1 and step < TILES - 1:
                 product(n - 1, range(PACK))
 
         last = BLOCKS - 1
-        w_before, w_last = 3, 4
-        transposed(last, w_before, nc.scalar.copy)
         quantised(last, 1)
-        row_sums(last)
-        normalised(last - 1)
+        transposed(last, 2, nc.vector.tensor_copy)
+        transposed(last, OWN, nc.vector.tensor_copy)
+        product(last - 1, range(PACK))
+        transposed(last, PACK - 1, nc.scalar.copy)
         quantised(last, 2)
+        quantised(last, OWN)
+        normalised(last - 1)
+        product(last, range(0, PACK - 1))
+        row_sums(last)
+        quantised(last, PACK - 1)
         reciprocals(last)
-        transposed(last, w_last, nc.vector.tensor_copy)
-        product(last, range(0, 2))
-        quantised(last, w_before)
-        quantised(last, w_last)
-        normalised(last, 0, 2)
-        product(last, range(2, PACK))
-        normalised(last, 2, PACK)
+        product(last, range(PACK - 1, PACK))
+        normalised(last, 0, PACK - 1)
+        normalised(last, PACK - 1, PACK)

@@ -55,7 +55,9 @@ def tile_exactslidingwindowattention_kernel(tc, q, k, v, out):
         for n in range(BLOCKS):
             nc.sync.dma_start(out=k_sb[:, n], in_=k_blocks[n])
             nc.sync.dma_start(out=q_sb[:, n], in_=q_blocks[n])
-            nc.sync.dma_start(out=v_sb[:, n], in_=v_blocks[n])
+            if n > 0:
+                nc.sync.dma_start(out=v_sb[:, n - 1], in_=v_blocks[n - 1])
+        nc.sync.dma_start(out=v_sb[:, BLOCKS - 1], in_=v_blocks[BLOCKS - 1])
 
         kT = keep.tile([D, S], BF16)
         qT = keep.tile([D, S], BF16)
@@ -121,7 +123,7 @@ def tile_exactslidingwindowattention_kernel(tc, q, k, v, out):
 
         def prepare_q(n):
             qT_n = qT[:].bitcast(F32)[:, n * BLOCK // 2:(n + 1) * BLOCK // 2]
-            if n == 0:
+            if n < 2:
                 nc.vector.tensor_copy(out=qT_n, in_=transposed_in(q_sb, n))
             else:
                 nc.scalar.copy(out=qT_n, in_=transposed_in(q_sb, n))
@@ -300,28 +302,36 @@ def tile_exactslidingwindowattention_kernel(tc, q, k, v, out):
         window_scores(0)
         window_scores(1)
         own_scores(0, range(first_own(0), PACK))
+        prepare_k(1)
+        window_maximum(0)
+        row_maximum(0)
+        own_maximum(0)
+        prepare_q(1)
         for step in range(TILES):
             n, r = divmod(step, PACK)
             if step + 2 < TILES:
                 window_scores(step + 2)
-            window_maximum(step)
-            for unit in units(step - 3):
-                quantised(*unit)
-            row_maximum(step)
+            if step > 0:
+                window_maximum(step)
+                for unit in units(step - 3):
+                    quantised(*unit)
+                row_maximum(step)
             if step == TILES - 1:
                 own_exponentials(step)
                 window_exponentials(step)
             else:
                 window_exponentials(step)
                 own_exponentials(step)
-            if step == 0:
-                own_maximum(0)
-                v_regrouped(0)
-                prepare_k(1)
             if step == 1:
+                v_regrouped(0)
+            if step == 2:
                 v_quantised(0)
                 v_rearranged(0)
-                prepare_q(1)
+            if step == 3:
+                v_regrouped(1)
+            if step == 4:
+                v_quantised(1)
+                v_rearranged(1)
             if step < TILES - 1:
                 for unit in units(step - 1):
                     transposed(*unit, nc.scalar.copy)
@@ -329,16 +339,15 @@ def tile_exactslidingwindowattention_kernel(tc, q, k, v, out):
                 normalised(n - 2)
             if r == 1 and n + 2 < BLOCKS:
                 prepare_k(n + 2)
-            if r == 0 and n + 1 < BLOCKS:
+            if r == 0 and 1 <= n < BLOCKS - 1:
                 v_regrouped(n + 1)
             if r == 1 and n >= 1:
                 row_sums(n - 1)
             if r == 2 and n + 2 < BLOCKS:
                 prepare_q(n + 2)
-            if r < 3 and n + 1 < BLOCKS:
-                shares = ([], [0, 1], [2, 3]) if n == 0 else ([0, 1], [2, 3], [])
-                own_scores(n + 1, shares[r])
-            if r == 2 and n + 1 < BLOCKS:
+            if r < 2 and n + 1 < BLOCKS:
+                own_scores(n + 1, range(2 * r, 2 * r + 2))
+            if r == 2 and 1 <= n < BLOCKS - 1:
                 v_quantised(n + 1)
                 v_rearranged(n + 1)
             if r == 2 and n >= 1:
@@ -350,9 +359,9 @@ def tile_exactslidingwindowattention_kernel(tc, q, k, v, out):
 
         last = BLOCKS - 1
         quantised(last, 1)
+        product(last - 1, range(PACK))
         transposed(last, 2, nc.vector.tensor_copy)
         transposed(last, OWN, nc.vector.tensor_copy)
-        product(last - 1, range(PACK))
         transposed(last, PACK - 1, nc.scalar.copy)
         quantised(last, 2)
         quantised(last, OWN)

@@ -130,7 +130,11 @@ def tile_exactslidingwindowattention_kernel(tc, q, k, v, out):
 
         def v_regrouped(n):
             v_grouped[n] = work.tile([P, D, PACK], BF16, name="v_grouped", align_bytes=64)
-            nc.vector.tensor_copy(out=v_grouped[n][:], in_=v_sb[:, n].rearrange("p t d -> p d t"))
+            for i in range(0, D, D // 4):
+                nc.gpsimd.tensor_scalar(
+                    out=v_grouped[n][:, i:i + D // 4, :],
+                    in0=v_sb[:, n, :, i:i + D // 4].rearrange("p t d -> p d t"),
+                    scalar1=1.0, scalar2=0.0, op0=ALU.mult, op1=ALU.add)
 
         def v_scales(row):
             return row[:, D:].bitcast(U8)
@@ -242,20 +246,22 @@ def tile_exactslidingwindowattention_kernel(tc, q, k, v, out):
             words = e_unit[n, w][:].rearrange("p u c -> p (u c)").bitcast(F32)
             for u in range(2):
                 nc.tensor.transpose(eT_ps[:, u, :], words[:, u * P:(u + 1) * P], ident_f32[:])
-            grouped[n, w] = work.tile([P, P, PACK], BF16, name="grouped", align_bytes=64)
+            if (n, w // 2) not in grouped:
+                grouped[n, w // 2] = work.tile([P, 2, P, PACK], BF16, name="grouped",
+                                               align_bytes=64)
             copy(
-                out=grouped[n, w][:].rearrange("p q t -> p (q t)").bitcast(F32).rearrange(
-                    "p (q u) -> p q u", u=2),
+                out=grouped[n, w // 2][:, w % 2].rearrange("p q t -> p (q t)").bitcast(
+                    F32).rearrange("p (q u) -> p q u", u=2),
                 in_=eT_ps[:].rearrange("p u q -> p q u"))
 
-        def quantised(n, w):
+        def quantised(n, w, count=1):
             if n not in e_codes:
                 e_codes[n] = per_block.tile([P, PACK + 1, P], U32, name="e_codes", align_bytes=64)
                 e_scales[n] = per_block.tile([P, PACK + 1, P], U8, name="e_scales", align_bytes=64)
             nc.vector.quantize_mx(
-                out=e_codes[n][:, w, :].bitcast(FP8X4),
-                scales=e_scales[n][:, w, :],
-                in_=grouped[n, w][:].rearrange("p q t -> p (q t)"),
+                out=e_codes[n][:, w:w + count, :].rearrange("p w q -> p (w q)").bitcast(FP8X4),
+                scales=e_scales[n][:, w:w + count, :].rearrange("p w q -> p (w q)"),
+                in_=grouped[n, w // 2][:, w % 2:w % 2 + count].rearrange("p w q t -> p (w q t)"),
             )
 
         def product(n, tiles):
@@ -284,7 +290,8 @@ def tile_exactslidingwindowattention_kernel(tc, q, k, v, out):
 
         def row_sums(n):
             den[n] = small.tile([P, PACK], F32, name="den")
-            nc.vector.tensor_reduce(out=den[n][:], in_=den_parts[:, n], axis=AXIS.X, op=ALU.add)
+            nc.gpsimd.tensor_tensor(out=den[n][:], in0=den_parts[:, n, :, 0],
+                                    in1=den_parts[:, n, :, 1], op=ALU.add)
 
         def reciprocals(n):
             inv_den[n] = small.tile([P, PACK], F32, name="inv_den")
@@ -313,8 +320,17 @@ def tile_exactslidingwindowattention_kernel(tc, q, k, v, out):
                 window_scores(step + 2)
             if step > 0:
                 window_maximum(step)
-                for unit in units(step - 3):
-                    quantised(*unit)
+                if r == 0 and n == 1:
+                    quantised(0, 1)
+                if r == 0 and n >= 2:
+                    quantised(n - 1, 0, 2)
+                if r == 1 and 1 <= n < BLOCKS - 1:
+                    v_quantised(n + 1)
+                    v_rearranged(n + 1)
+                if r == 2 and n >= 1:
+                    quantised(n - 1, OWN)
+                if r == 3 and n >= 1:
+                    quantised(n - 1, 2, 2)
                 row_maximum(step)
             if step == TILES - 1:
                 own_exponentials(step)
@@ -347,9 +363,6 @@ def tile_exactslidingwindowattention_kernel(tc, q, k, v, out):
                 prepare_q(n + 2)
             if r < 2 and n + 1 < BLOCKS:
                 own_scores(n + 1, range(2 * r, 2 * r + 2))
-            if r == 2 and 1 <= n < BLOCKS - 1:
-                v_quantised(n + 1)
-                v_rearranged(n + 1)
             if r == 2 and n >= 1:
                 reciprocals(n - 1)
             if r == 3 and n + 1 < BLOCKS:
@@ -358,7 +371,7 @@ def tile_exactslidingwindowattention_kernel(tc, q, k, v, out):
                 product(n - 1, range(PACK))
 
         last = BLOCKS - 1
-        quantised(last, 1)
+        quantised(last, 0, 2)
         product(last - 1, range(PACK))
         transposed(last, 2, nc.vector.tensor_copy)
         transposed(last, OWN, nc.vector.tensor_copy)

from contextlib import ExitStack

import concourse.mybir as mybir
from concourse.masks import make_identity

F32 = mybir.dt.float32
BF16 = mybir.dt.bfloat16
U32 = mybir.dt.uint32
I32 = mybir.dt.int32
U8 = mybir.dt.uint8
FP8X4 = mybir.dt.float8_e4m3fn_x4
ALU = mybir.AluOpType
ACT = mybir.ActivationFunctionType
AXIS = mybir.AxisListType

P = 128
S = 4096
D = 128
PACK = 4
BLOCK = PACK * P
SLOT = P // PACK
TILES = S // P
BLOCKS = S // BLOCK
HALF = P // 2
OWN = PACK
V_ROW = D + D // 4
V_RING = 4
SCALE = D ** -0.5
MASKED = -3.0e38

FLOPS = 2 * (2 * BLOCKS - 1) * 2 * BLOCK * BLOCK * D


def tile_exactslidingwindowattention_kernel(tc, q, k, v, out):
    nc = tc.nc
    q_blocks = q.flatten_outer_dims().rearrange("(n t p) d -> n p t d", t=PACK, p=P)
    k_blocks = k.flatten_outer_dims().rearrange("(n t p) d -> n p t d", t=PACK, p=P)
    v_blocks = v.flatten_outer_dims().rearrange("(n p t) d -> n p t d", t=PACK, p=P)
    out_blocks = out.flatten_outer_dims().rearrange("(n t p) d -> n p t d", t=PACK, p=P)

    with ExitStack() as ctx:
        ctx.enter_context(tc.manual_schedule())
        keep = ctx.enter_context(tc.tile_pool(name="keep", bufs=1))
        work = ctx.enter_context(tc.tile_pool(name="work", bufs=4))
        per_block = ctx.enter_context(tc.tile_pool(name="per_block", bufs=2))
        small = ctx.enter_context(tc.tile_pool(name="small", bufs=4))
        psum_window = ctx.enter_context(tc.psum_pool(name="psum_window", bufs=3))
        psum_own = ctx.enter_context(tc.psum_pool(name="psum_own", bufs=2))
        psum_turns = ctx.enter_context(tc.psum_pool(name="psum_turns", bufs=2))
        psum_num = ctx.enter_context(tc.psum_pool(name="psum_num", bufs=1))

        q_sb = keep.tile([P, BLOCKS, PACK, D], BF16)
        k_sb = keep.tile([P, BLOCKS, PACK, D], BF16)
        v_sb = keep.tile([P, BLOCKS, PACK, D], BF16)
        for n in range(BLOCKS):
            nc.sync.dma_start(out=k_sb[:, n], in_=k_blocks[n])
            nc.sync.dma_start(out=q_sb[:, n], in_=q_blocks[n])
            if n > 0:
                nc.sync.dma_start(out=v_sb[:, n - 1], in_=v_blocks[n - 1])
        nc.sync.dma_start(out=v_sb[:, BLOCKS - 1], in_=v_blocks[BLOCKS - 1])

        kT = keep.tile([D, S], BF16)
        qT = keep.tile([D, S], BF16)
        v_mx = keep.tile([P, BLOCKS, V_ROW], U32, align_bytes=64)
        v_slot = []
        for i in range(V_RING):
            v_slot_i = keep.tile([P, PACK, D], U32, name="v_slot%d" % i, align_bytes=64)
            nc.vector.memset(v_slot_i[:], 0)
            v_slot.append(v_slot_i)

        ident = keep.tile([P, P], BF16)
        make_identity(nc, ident[:])
        mask_own = keep.tile([P, P], BF16)
        nc.gpsimd.memset(mask_own[:], 0.0)
        nc.gpsimd.affine_select(
            out=mask_own[:], in_=mask_own[:], compare_op=ALU.is_ge, fill=MASKED,
            base=0, pattern=[[-1, P]], channel_multiplier=1,
        )
        mask_prev = keep.tile([P, P], BF16)
        nc.gpsimd.memset(mask_prev[:], 0.0)
        nc.gpsimd.affine_select(
            out=mask_prev[:], in_=mask_prev[:], compare_op=ALU.is_ge, fill=MASKED,
            base=-1, pattern=[[1, P]], channel_multiplier=-1,
        )
        ident_f32 = keep.tile([P, P], F32)
        make_identity(nc, ident_f32[:])

        nc.gpsimd.memset(v_mx[:, :, D:], 0)
        e_first = {}
        for T in range(1, PACK):
            e_first[T] = keep.tile([P, 2, PACK * HALF], BF16, name="e_first%d" % T)
            nc.gpsimd.memset(e_first[T][:], 0.0)
        den_parts = keep.tile([P, BLOCKS, PACK, 2], F32)
        nc.gpsimd.memset(den_parts[:], 0.0)

        own_ps = {}
        own_max = {}
        window_ps = {}
        window_max = {}
        neg_max = {}
        v_grouped = {}
        v_window = {}
        den = {}
        inv_den = {}
        num_ps = {}
        e_unit = {}
        grouped = {}
        e_codes = {}
        e_scales = {}

        def window_tiles(T):
            return min(T, PACK)

        def transposed_in(x_sb, n):
            x_ps = psum_turns.tile([D, PACK, P], BF16, name="x_ps", tag="turns")
            for t in range(PACK):
                nc.tensor.transpose(x_ps[:, t, :], x_sb[:, n, t, :], ident[:])
            return x_ps[:].rearrange("d t p -> d (t p)").bitcast(F32)

        def prepare_k(n):
            nc.scalar.copy(out=kT[:].bitcast(F32)[:, n * BLOCK // 2:(n + 1) * BLOCK // 2],
                           in_=transposed_in(k_sb, n))

        def prepare_q(n):
            qT_n = qT[:].bitcast(F32)[:, n * BLOCK // 2:(n + 1) * BLOCK // 2]
            if n < 2:
                nc.vector.tensor_copy(out=qT_n, in_=transposed_in(q_sb, n))
            else:
                nc.scalar.copy(out=qT_n, in_=transposed_in(q_sb, n))

        def v_regrouped(n):
            v_grouped[n] = work.tile([P, D, PACK], BF16, name="v_grouped", align_bytes=64)
            for i in range(0, D, D // 4):
                nc.gpsimd.tensor_scalar(
                    out=v_grouped[n][:, i:i + D // 4, :],
                    in0=v_sb[:, n, :, i:i + D // 4].rearrange("p t d -> p d t"),
                    scalar1=1.0, scalar2=0.0, op0=ALU.mult, op1=ALU.add)

        def v_scales(row):
            return row[:, D:].bitcast(U8)

        def v_quantised(n):
            nc.vector.quantize_mx(
                out=v_mx[:, n, 0:D].bitcast(FP8X4),
                scales=v_scales(v_mx[:, n]),
                in_=v_grouped[n][:].rearrange("p d t -> p (d t)"),
            )

        def v_rearranged(n):
            for s in range(PACK):
                rows = slice(s * SLOT, (s + 1) * SLOT)
                nc.sync.dma_start(out=v_slot[n % V_RING][rows, s, :].bitcast(I32),
                                  in_=v_mx[rows, n, 0:D].bitcast(I32))
            if n == 0:
                return
            v_window[n] = work.tile([P, PACK - 1, V_ROW], U32, name="v_window",
                                    align_bytes=64)
            for r in range(1, PACK):
                cut = (PACK - r) * SLOT
                nc.sync.dma_start(out=v_window[n][0:cut, r - 1, :].bitcast(I32),
                                  in_=v_mx[P - cut:P, n - 1, :].bitcast(I32))
                nc.sync.dma_start(out=v_window[n][cut:P, r - 1, :].bitcast(I32),
                                  in_=v_mx[0:P - cut, n, :].bitcast(I32))

        def own_tile_scores(T, out):
            nc.tensor.matmul(out=out, lhsT=qT[:, T * P:(T + 1) * P],
                             rhs=kT[:, T * P:(T + 1) * P], start=True, stop=False)
            nc.tensor.matmul(out=out, lhsT=ident[:], rhs=mask_own[:], start=False, stop=True)

        def first_own(n):
            return 1 if n == 0 else 0

        def own_scores(n, tiles):
            if n not in own_ps:
                own_ps[n] = psum_own.tile([P, PACK, P], F32, name="own_ps")
            for r in tiles:
                own_tile_scores(n * PACK + r, own_ps[n][:, r, :])

        def own_maximum(n):
            r0 = first_own(n)
            own_max[n] = small.tile([P, PACK], F32, name="own_max")
            nc.vector.tensor_reduce(out=own_max[n][:, r0:], in_=own_ps[n][:, r0:, :],
                                    axis=AXIS.X, op=ALU.max)

        def window_scores(T):
            count = window_tiles(T)
            window_ps[T] = psum_window.tile([P, BLOCK], F32, name="window_ps")
            if T == 0:
                own_tile_scores(T, window_ps[T][:, 0:P])
                return
            clipped = count == PACK
            nc.tensor.matmul(out=window_ps[T][:, 0:count * P],
                             lhsT=qT[:, T * P:(T + 1) * P],
                             rhs=kT[:, (T - count) * P:T * P],
                             start=True, stop=not clipped)
            if clipped:
                nc.tensor.matmul(out=window_ps[T][:, 0:P], lhsT=ident[:], rhs=mask_prev[:],
                                 start=False, stop=True)

        def window_maximum(T):
            window_max[T] = small.tile([P, 1], F32, name="window_max")
            nc.vector.tensor_reduce(out=window_max[T][:],
                                    in_=window_ps[T][:, 0:max(window_tiles(T), 1) * P],
                                    axis=AXIS.X, op=ALU.max)

        def row_maximum(T):
            n, r = divmod(T, PACK)
            neg_max[T] = small.tile([P, 1], F32, name="neg_max")
            if T > 0:
                nc.vector.tensor_scalar(out=neg_max[T][:], in0=window_max[T][:],
                                        scalar1=own_max[n][:, r:r + 1], scalar2=-SCALE,
                                        op0=ALU.max, op1=ALU.mult)
            else:
                nc.vector.tensor_scalar(out=neg_max[T][:], in0=window_max[T][:],
                                        scalar1=-SCALE, scalar2=None, op0=ALU.mult)

        def exponentials(T, scores, e_out, part):
            n, r = divmod(T, PACK)
            nc.scalar.activation(out=e_out.rearrange("p u (w e) -> p u w e", e=2),
                                 in_=scores.rearrange("p (w u e) -> p u w e", u=2, e=2),
                                 func=ACT.Exp, bias=neg_max[T][:], scale=SCALE,
                                 accum_out=den_parts[:, n, r, part:part + 1])

        def window_exponentials(T):
            n, r = divmod(T, PACK)
            if T == 0:
                return
            count = window_tiles(T)
            e_unit[n, r] = e_first[T] if T in e_first else work.tile(
                [P, 2, PACK * HALF], BF16, name="e_window")
            exponentials(T, window_ps[T][:, 0:count * P], e_unit[n, r][:, :, 0:count * HALF], 0)

        def own_exponentials(T):
            n, r = divmod(T, PACK)
            if r == 0:
                e_unit[n, OWN] = per_block.tile([P, 2, PACK * HALF], BF16, name="e_own")
            exponentials(T, own_ps[n][:, r, :] if T > 0 else window_ps[T][:, 0:P],
                         e_unit[n, OWN][:, :, r * HALF:(r + 1) * HALF], 1)

        def units(T):
            n, r = divmod(T, PACK)
            return ([(n, r)] if T > 0 else []) + ([(n, OWN)] if r == PACK - 1 and T > 0 else [])

        def transposed(n, w, copy):
            eT_ps = psum_turns.tile([P, 2, P], F32, name="eT_ps", tag="turns")
            words = e_unit[n, w][:].rearrange("p u c -> p (u c)").bitcast(F32)
            for u in range(2):
                nc.tensor.transpose(eT_ps[:, u, :], words[:, u * P:(u + 1) * P], ident_f32[:])
            if (n, w // 2) not in grouped:
                grouped[n, w // 2] = work.tile([P, 2, P, PACK], BF16, name="grouped",
                                               align_bytes=64)
            copy(
                out=grouped[n, w // 2][:, w % 2].rearrange("p q t -> p (q t)").bitcast(
                    F32).rearrange("p (q u) -> p q u", u=2),
                in_=eT_ps[:].rearrange("p u q -> p q u"))

        def quantised(n, w, count=1):
            if n not in e_codes:
                e_codes[n] = per_block.tile([P, PACK + 1, P], U32, name="e_codes", align_bytes=64)
                e_scales[n] = per_block.tile([P, PACK + 1, P], U8, name="e_scales", align_bytes=64)
            nc.vector.quantize_mx(
                out=e_codes[n][:, w:w + count, :].rearrange("p w q -> p (w q)").bitcast(FP8X4),
                scales=e_scales[n][:, w:w + count, :].rearrange("p w q -> p (w q)"),
                in_=grouped[n, w // 2][:, w % 2:w % 2 + count].rearrange("p w q t -> p (w q t)"),
            )

        def product(n, tiles):
            if n < BLOCKS - 1:
                sums = psum_num.tile([P, PACK, D], F32, name="num_ps")
            else:
                sums = psum_window.tile([P, PACK, D], F32, name="num_ps", tag="window_ps")
            for r in tiles:
                num_ps[n, r] = sums
                operands = [(OWN, v_slot[n % V_RING][:, r, :], v_scales(v_mx[:, n]))]
                if n == 0 and r > 0:
                    operands.append((r, v_mx[:, 0, 0:D], v_scales(v_mx[:, 0])))
                if n > 0:
                    row = v_mx[:, n - 1] if r == 0 else v_window[n][:, r - 1]
                    operands.append((r, row[:, 0:D], v_scales(row)))
                for i, (w, codes, scales) in enumerate(operands):
                    nc.tensor.matmul_mx(
                        out=sums[:, r, :],
                        lhsT=e_codes[n][:, w, :].bitcast(FP8X4),
                        lhsT_scale=e_scales[n][:, w, :],
                        rhs=codes.bitcast(FP8X4),
                        rhs_scale=scales,
                        start=(i == 0),
                        stop=(i == len(operands) - 1),
                    )

        def row_sums(n):
            den[n] = small.tile([P, PACK], F32, name="den")
            nc.gpsimd.tensor_tensor(out=den[n][:], in0=den_parts[:, n, :, 0],
                                    in1=den_parts[:, n, :, 1], op=ALU.add)

        def reciprocals(n):
            inv_den[n] = small.tile([P, PACK], F32, name="inv_den")
            nc.vector.reciprocal(out=inv_den[n][:], in_=den[n][:])

        def normalised(n, r0=0, r1=PACK):
            out_sb = work.tile([P, PACK, D], F32, name="out_sb")
            nc.vector.tensor_tensor(
                out=out_sb[:, r0:r1, :], in0=num_ps[n, r0][:, r0:r1, :],
                in1=inv_den[n][:, r0:r1].unsqueeze(2).to_broadcast([P, r1 - r0, D]), op=ALU.mult)
            nc.sync.dma_start(out=out_blocks[n][:, r0:r1, :], in_=out_sb[:, r0:r1, :])

        prepare_k(0)
        prepare_q(0)
        window_scores(0)
        window_scores(1)
        own_scores(0, range(first_own(0), PACK))
        prepare_k(1)
        window_maximum(0)
        row_maximum(0)
        own_maximum(0)
        prepare_q(1)
        for step in range(TILES):
            n, r = divmod(step, PACK)
            if step + 2 < TILES:
                window_scores(step + 2)
            if step > 0:
                window_maximum(step)
                if r == 0 and n == 1:
                    quantised(0, 1)
                if r == 0 and n >= 2:
                    quantised(n - 1, 0, 2)
                if r == 1 and 1 <= n < BLOCKS - 1:
                    v_quantised(n + 1)
                    v_rearranged(n + 1)
                if r == 2 and n >= 1:
                    quantised(n - 1, OWN)
                if r == 3 and n >= 1:
                    quantised(n - 1, 2, 2)
                row_maximum(step)
            if step == TILES - 1:
                own_exponentials(step)
                window_exponentials(step)
            else:
                window_exponentials(step)
                own_exponentials(step)
            if step == 1:
                v_regrouped(0)
            if step == 2:
                v_quantised(0)
                v_rearranged(0)
            if step == 3:
                v_regrouped(1)
            if step == 4:
                v_quantised(1)
                v_rearranged(1)
            if step < TILES - 1:
                for unit in units(step - 1):
                    transposed(*unit, nc.scalar.copy)
            if r == 1 and n >= 2:
                normalised(n - 2)
            if r == 1 and n + 2 < BLOCKS:
                prepare_k(n + 2)
            if r == 0 and 1 <= n < BLOCKS - 1:
                v_regrouped(n + 1)
            if r == 1 and n >= 1:
                row_sums(n - 1)
            if r == 2 and n + 2 < BLOCKS:
                prepare_q(n + 2)
            if r < 2 and n + 1 < BLOCKS:
                own_scores(n + 1, range(2 * r, 2 * r + 2))
            if r == 2 and n >= 1:
                reciprocals(n - 1)
            if r == 3 and n + 1 < BLOCKS:
                own_maximum(n + 1)
            if r == 3 and n >= 1 and step < TILES - 1:
                product(n - 1, range(PACK))

        last = BLOCKS - 1
        quantised(last, 0, 2)
        product(last - 1, range(PACK))
        transposed(last, 2, nc.vector.tensor_copy)
        transposed(last, OWN, nc.vector.tensor_copy)
        transposed(last, PACK - 1, nc.scalar.copy)
        quantised(last, 2)
        quantised(last, OWN)
        normalised(last - 1)
        product(last, range(0, PACK - 1))
        row_sums(last)
        quantised(last, PACK - 1)
        reciprocals(last)
        product(last, range(PACK - 1, PACK))
        normalised(last, 0, PACK - 1)
        normalised(last, PACK - 1, PACK)
